import numpy as np
import ml_dtypes


def mxq(x, axis, fmt="e4m3"):
    dtype, down = {"e4m3": (ml_dtypes.float8_e4m3fn, 7), "e5m2": (ml_dtypes.float8_e5m2, 14)}[fmt]
    v = np.moveaxis(np.asarray(x, np.float32).astype(ml_dtypes.bfloat16).astype(np.float64), axis, -1)
    blocks = v.reshape(v.shape[:-1] + (-1, 32))
    amax = np.abs(blocks).max(-1, keepdims=True)
    byte = np.maximum(np.where(amax > 0, np.frexp(amax)[1] - 1 + 127, 0) - down, 1)
    scale = np.exp2(byte - 127.0)
    codes = (blocks / scale).astype(np.float32).astype(dtype).astype(np.float64)
    return np.moveaxis((codes * scale).reshape(v.shape), -1, axis)


WIDE = False


def mx_kscale(k):
    if not WIDE:
        return np.ones(k)
    levels = np.array([10, -10, 5, -5, 0])
    a = np.random.permutation(np.resize(levels, k // 512 * 4)).reshape(k // 512, 4)
    idx = np.arange(k)
    return np.exp2(a[idx // 512, idx % 128 // 32])


BF16 = ml_dtypes.bfloat16


def bf(x):
    return np.asarray(x, np.float32).astype(BF16)


def f64(x):
    return np.asarray(x).astype(np.float64)


B, T, C, F = 4, 512, 512, 2048
M = T
K = C + C


def silu(v):
    return v / (1.0 + np.exp(-v))


def setup_inputs():
    s = mx_kscale(K)
    u = s[:C]
    x = np.random.standard_normal((B, T, C)) + 0.5 * np.random.standard_normal((B, 1, C))
    return {"x": bf(x * u),
            "memory": bf(np.random.standard_normal((1, M, C)) * 6.0 / np.sqrt(C) / u),
            "w1": bf(np.random.standard_normal((K, F)) / np.sqrt(K) * np.concatenate([1.0 / u, u])[:, None]),
            "b1": bf(np.random.standard_normal(F) * 0.3)}


def reference(x, memory, w1, b1):
    energy = f64(x) @ f64(memory)[0].T
    e = np.exp(energy - energy.max(-1, keepdims=True))
    retrieved = (mxq(e, 2, "e4m3") @ mxq(f64(memory)[0], 0, "e4m3")) / e.sum(-1, keepdims=True)
    cat = np.concatenate([f64(x), retrieved], axis=-1)
    return silu((mxq(cat, 2, "e4m3") @ mxq(f64(w1), 0, "e4m3")) + f64(b1))

@@ -1,0 +1,384 @@
+from contextlib import ExitStack
+
+import concourse.mybir as mybir
+from concourse.masks import make_identity
+
+F32 = mybir.dt.float32
+BF16 = mybir.dt.bfloat16
+U32 = mybir.dt.uint32
+U8 = mybir.dt.uint8
+FP8X4 = mybir.dt.float8_e4m3fn_x4
+ACT = mybir.ActivationFunctionType
+ALU = mybir.AluOpType
+AX = mybir.AxisListType
+
+P = 128
+TOKENS = 2048
+C = 512
+SLOTS = 512
+F = 2048
+NT = TOKENS // P
+HALF = F // 2
+FLOPS = 2 * TOKENS * C * SLOTS * 2 + 2 * TOKENS * 2 * C * F
+PIN = True
+
+
+def tile_dynamicmemorybank_pa_kernel(tc, x, memory, w1, b1, out):
+    nc = tc.nc
+    with ExitStack() as ctx:
+        keep = ctx.enter_context(tc.tile_pool(name="keep", bufs=1))
+        ring = ctx.enter_context(tc.tile_pool(name="ring", bufs=2))
+        psum = ctx.enter_context(tc.psum_pool(name="psum", bufs=1))
+        if PIN:
+            ctx.enter_context(tc.manual_schedule())
+
+        x_v = x.flatten_outer_dims().rearrange("(p i) c -> p i c", i=NT)
+        out_v = out.flatten_outer_dims().rearrange("(p i) f -> p i f", i=NT)
+        mem_v = memory.flatten_outer_dims().rearrange("(p j) c -> p j c", j=4)
+
+        count = [0]
+
+        def bank(k, shape, dtype):
+            count[0] += 1
+            return psum.tile(shape, dtype, tag="bank%d" % k, name="ps%d" % count[0])
+
+        ident_f = keep.tile([P, P], F32, name="ident_f")
+        ident_b = keep.tile([P, P], BF16, name="ident_b")
+        make_identity(nc, ident_f[:])
+        make_identity(nc, ident_b[:])
+
+        mem_sb = keep.tile([P, 4 * C], BF16, name="mem_sb")
+        mem_t = keep.tile([P, 2 * SLOTS], F32, name="mem_t")
+        mem_g = keep.tile([P, 4 * C], BF16, name="mem_g", align_bytes=64)
+        mem_c = keep.tile([P, C], U32, name="mem_c", align_bytes=64)
+        mem_s = keep.tile([P, C], U8, name="mem_s", align_bytes=64)
+        x_sb = [keep.tile([P, 4 * C], BF16, name="x_sb%d" % g) for g in range(4)]
+        x_g = keep.tile([P, NT * P * 4], BF16, name="x_g", tag="big", align_bytes=64)
+        x_c = keep.tile([P, TOKENS], U32, name="x_c", align_bytes=64)
+        x_s = keep.tile([P, TOKENS], U8, name="x_s", align_bytes=64)
+        r_c = keep.tile([P, TOKENS], U32, name="r_c", align_bytes=64)
+        r_s = keep.tile([P, TOKENS], U8, name="r_s", align_bytes=64)
+        negmax = keep.tile([P, NT], F32, name="negmax")
+        rowsum = keep.tile([P, NT], F32, name="rowsum")
+        recip = keep.tile([P, NT], F32, name="recip")
+        bias = keep.tile([P, F], BF16, name="bias")
+        w_raw = {}
+        w_c = {}
+        w_s = {}
+        for h in range(2):
+            for g in range(2):
+                w_raw[g, h] = keep.tile([P, 4 * HALF], BF16, name="w_raw%d%d" % (g, h))
+                w_c[g, h] = keep.tile([P, HALF], U32, name="w_c%d%d" % (g, h), align_bytes=64)
+                w_s[g, h] = keep.tile([P, HALF], U8, name="w_s%d%d" % (g, h), align_bytes=64)
+
+        x_gw = x_g[:].bitcast(F32).rearrange("p (i r u) -> p i r u", i=NT, r=P, u=2)
+        x_gb = x_g[:].rearrange("p (i r t) -> p i r t", i=NT, r=P, t=4)
+        mem_tb = mem_t[:].bitcast(BF16).rearrange("p (u c e) -> p u c e", u=2, e=2)
+
+        def load_w(g, h):
+            cols = slice(h * HALF, (h + 1) * HALF)
+            dst = w_raw[g, h][:].rearrange("p (t f) -> p t f", t=4)
+            if g == 0:
+                for u in range(2):
+                    nc.sync.dma_start(
+                        out=dst[:, 2 * u : 2 * u + 2, :],
+                        in_=w1[256 * u : 256 * u + 256, cols].rearrange("(q e) f -> q e f", e=2),
+                    )
+            else:
+                nc.sync.dma_start(out=dst, in_=w1[C : 2 * C, cols].rearrange("(p j) f -> p j f", j=4))
+
+        def load_x(g):
+            nc.sync.dma_start(
+                out=x_sb[g][:].rearrange("p (i c) -> p i c", i=4), in_=x_v[:, 4 * g : 4 * g + 4, :]
+            )
+
+        nc.sync.dma_start(out=mem_sb[:].rearrange("p (j c) -> p j c", j=4), in_=mem_v)
+        load_x(0)
+        load_w(0, 0)
+        load_x(1)
+        load_w(1, 0)
+        load_x(2)
+        load_w(0, 1)
+        load_x(3)
+        load_w(1, 1)
+        nc.sync.dma_start(out=bias[:], in_=b1.partition_broadcast(P))
+
+        xt_ps = {}
+        et_ps = {}
+        rt_ps = {}
+        e_sb = {}
+        e_g = {}
+        e_c = {}
+        e_s = {}
+        r_b = {}
+        r_g = {}
+        m2_ps = {}
+
+        def pe_xt(k, which, b=2):
+            if which == 0:
+                xt_ps[k] = bank(b, [P, 2, 2, P], F32)
+            a, u = divmod(which, 2)
+            i = 2 * k + a
+            src = x_sb[i // 4][:].bitcast(F32).rearrange("p (i w) -> p i w", i=4)
+            nc.tensor.transpose(xt_ps[k][:, a, u, :], src[:, i % 4, P * u : P * u + P], ident_f[:])
+
+        def evac_xt(eng_copy, k):
+            eng_copy(out=x_gw[:, 2 * k : 2 * k + 2, :, :], in_=xt_ps[k][:].rearrange("p a u r -> p a r u"))
+
+        def v_qx(g):
+            cols = slice(512 * g, 512 * g + 512)
+            nc.vector.quantize_mx(
+                out=x_c[:, cols].bitcast(FP8X4), scales=x_s[:, cols], in_=x_g[:, 2048 * g : 2048 * g + 2048]
+            )
+
+        def pe_et(k, which):
+            if which == 0:
+                et_ps[k] = bank(3 + k % 2, [P, 2, 4, P], BF16)
+            a, t = divmod(which, 4)
+            nc.tensor.transpose(et_ps[k][:, a, t, :], e_sb[2 * k + a][:, P * t : P * t + P], ident_b[:])
+
+        def s_evac_et(k):
+            e_g[k] = ring.tile([P, 2 * P * 4], BF16, name="e_g", align_bytes=64)
+            nc.scalar.copy(
+                out=e_g[k][:].rearrange("p (a r t) -> p a r t", a=2, r=P, t=4),
+                in_=et_ps[k][:].rearrange("p a t r -> p a r t"),
+            )
+
+        def v_qe(k):
+            e_c[k] = ring.tile([P, 2 * P], U32, name="e_c", align_bytes=64)
+            e_s[k] = ring.tile([P, 2 * P], U8, name="e_s", align_bytes=64)
+            nc.vector.quantize_mx(out=e_c[k][:].bitcast(FP8X4), scales=e_s[k][:], in_=e_g[k][:])
+
+        def v_recip(k):
+            nc.vector.reciprocal(out=recip[:, 2 * k : 2 * k + 2], in_=rowsum[:, 2 * k : 2 * k + 2])
+
+        def pe_rt(k, a):
+            if a == 0:
+                rt_ps[k] = bank(3 if k == 7 else 5, [P, 2, P], F32)
+            i = 2 * k + a
+            nc.tensor.transpose(rt_ps[k][:, a, :], recip[:, i : i + 1].to_broadcast([P, P]), ident_f[:])
+
+        def s_evac_rt(k):
+            r_b[k] = ring.tile([P, 2, P], F32, name="r_b", bufs=3)
+            nc.scalar.copy(out=r_b[k][:], in_=rt_ps[k][:])
+
+        def pe_m2(i):
+            k, a = divmod(i, 2)
+            m2_ps[i] = bank(6 + i % 2, [P, 4, P], F32)
+            for q in range(4):
+                nc.tensor.matmul_mx(
+                    out=m2_ps[i][:, q, :],
+                    lhsT=mem_c[:, P * q : P * q + P].bitcast(FP8X4),
+                    lhsT_scale=mem_s[:, P * q : P * q + P],
+                    rhs=e_c[k][:, P * a : P * a + P].bitcast(FP8X4),
+                    rhs_scale=e_s[k][:, P * a : P * a + P],
+                    start=True,
+                    stop=True,
+                )
+
+        def v_rg(i):
+            k, a = divmod(i, 2)
+            if a == 0:
+                r_g[k] = ring.tile([P, 2 * P * 4], BF16, name="r_g", align_bytes=64)
+            dst = r_g[k][:].rearrange("p (a r q) -> p a r q", a=2, r=P, q=4)
+            nc.vector.tensor_tensor(
+                out=dst[:, a, :, :],
+                in0=m2_ps[i][:].rearrange("p q r -> p r q"),
+                in1=r_b[k][:, a, :].unsqueeze(2).to_broadcast([P, P, 4]),
+                op=ALU.mult,
+            )
+
+        def v_qr(k):
+            cols = slice(256 * k, 256 * k + 256)
+            nc.vector.quantize_mx(out=r_c[:, cols].bitcast(FP8X4), scales=r_s[:, cols], in_=r_g[k][:])
+
+        w_g = {}
+        w_g00 = keep.tile([P, 4 * HALF], BF16, name="w_g00", align_bytes=64)
+        w_g10 = keep.tile([P, 4 * HALF], BF16, name="w_g10", align_bytes=64)
+        w_g[0, 0] = w_g00[:]
+        w_g[1, 0] = w_g10[:]
+
+        def regroup_w(eng, g, h, piece, pieces):
+            n = HALF // pieces
+            cols = slice(n * piece, n * piece + n)
+            if eng == "g":
+                nc.gpsimd.tensor_scalar(
+                    out=w_g[g, h].rearrange("p (f t) -> p f t", t=4)[:, cols, :],
+                    in0=w_raw[g, h][:].rearrange("p (t f) -> p f t", t=4)[:, cols, :],
+                    scalar1=1.0,
+                    scalar2=0.0,
+                    op0=ALU.mult,
+                    op1=ALU.add,
+                )
+            else:
+                dst = w_g[g, h].rearrange("p (f t) -> p f t", t=4)[:, cols, :].rearrange("p (c i) t -> p c t i", i=4)
+                src = w_raw[g, h][:].rearrange("p (t f) -> p t f", t=4)[:, :, cols].rearrange("p t (c i) -> p c t i", i=4)
+                if eng == "v":
+                    nc.vector.tensor_copy(out=dst, in_=src)
+                else:
+                    nc.scalar.copy(out=dst, in_=src)
+
+        def v_qw(g, h):
+            nc.vector.quantize_mx(out=w_c[g, h][:].bitcast(FP8X4), scales=w_s[g, h][:], in_=w_g[g, h])
+
+        acc_count = [0]
+
+        def m3(h, i, banks, split):
+            v = ring.tile([P, HALF], F32, name="v", bufs=6)
+            for fc in range(2):
+                acc = bank(banks[acc_count[0] % len(banks)], [P, 512], F32)
+                acc_count[0] += 1
+                cols = slice(512 * fc, 512 * fc + 512)
+                toks = slice(P * i, P * i + P)
+                nc.tensor.matmul_mx(
+                    out=acc[:],
+                    lhsT=x_c[:, toks].bitcast(FP8X4),
+                    lhsT_scale=x_s[:, toks],
+                    rhs=w_c[0, h][:, cols].bitcast(FP8X4),
+                    rhs_scale=w_s[0, h][:, cols],
+                    start=True,
+                    stop=False,
+                )
+                nc.tensor.matmul_mx(
+                    out=acc[:],
+                    lhsT=r_c[:, toks].bitcast(FP8X4),
+                    lhsT_scale=r_s[:, toks],
+                    rhs=w_c[1, h][:, cols].bitcast(FP8X4),
+                    rhs_scale=w_s[1, h][:, cols],
+                    start=False,
+                    stop=True,
+                )
+                nc.vector.tensor_tensor(
+                    out=v[:, cols], in0=acc[:], in1=bias[:, h * HALF + 512 * fc : h * HALF + 512 * fc + 512], op=ALU.add
+                )
+                if split:
+                    nc.scalar.activation(out=v[:, cols], in_=v[:, cols], func=ACT.Silu)
+                    nc.sync.dma_start(
+                        out=out_v[:, i, h * HALF + 512 * fc : h * HALF + 512 * fc + 512], in_=v[:, cols]
+                    )
+            if not split:
+                nc.scalar.activation(out=v[:], in_=v[:], func=ACT.Silu)
+                nc.sync.dma_start(out=out_v[:, i, h * HALF : (h + 1) * HALF], in_=v[:])
+
+        warm = keep.tile([P, 2], F32, name="warm")
+        nc.vector.memset(warm[:], 0.0)
+        nc.scalar.activation(out=warm[:, 0:1], in_=warm[:, 1:2], func=ACT.Exp)
+        mem_w = mem_sb[:].bitcast(F32).rearrange("p (j w) -> p j w", j=4)
+        for u in range(2):
+            mt = bank(u, [P, 4, P], F32)
+            for j in range(4):
+                nc.tensor.transpose(mt[:, j, :], mem_w[:, j, P * u : P * u + P], ident_f[:])
+            dst = mem_t[:, SLOTS * u : SLOTS * u + SLOTS]
+            if u == 0:
+                nc.scalar.copy(out=dst, in_=mt[:].rearrange("p j r -> p (j r)"))
+            else:
+                nc.vector.tensor_copy(out=dst, in_=mt[:].rearrange("p j r -> p (j r)"))
+        nc.gpsimd.tensor_scalar(
+            out=mem_g[:].rearrange("p (q m j) -> p q m j", q=4, m=P, j=4),
+            in0=mem_sb[:].rearrange("p (j m q) -> p q m j", j=4, m=P, q=4),
+            scalar1=1.0,
+            scalar2=0.0,
+            op0=ALU.mult,
+            op1=ALU.add,
+        )
+        for k in range(2):
+            for which in range(4):
+                pe_xt(k, which, 2 + k)
+            evac_xt(nc.scalar.copy if k == 0 else nc.vector.tensor_copy, k)
+
+        V_FILL = {3: [(1, 0)], 4: [(1, 1)]}
+        S_FILL = {3: [(1, 2)], 5: [(1, 3)]}
+        QW_TICK = {7: (0, 0), 9: (1, 0), 22: (0, 1), 27: (1, 1)}
+        QX_TICK = {5: 0, 6: 1, 10: 2, 14: 3}
+        QMEM_TICK = 5
+        for piece in range(4):
+            regroup_w("g", 0, 0, piece, 4)
+        BUNCH = 18
+        units = [(h, i) for h in range(2) for i in range(NT)]
+        for tick in range(NT + len(units)):
+            if tick % 2 == 0 and 0 <= (tick - 4) // 2 <= 6:
+                s_evac_et((tick - 4) // 2)
+            if tick == NT:
+                nc.scalar.activation(out=warm[:, 0:1], in_=warm[:, 1:2], func=ACT.Silu)
+            for g, piece in S_FILL.get(tick, []):
+                regroup_w("s", g, 0, piece, 4)
+            if tick in QX_TICK:
+                v_qx(QX_TICK[tick])
+            if tick == QMEM_TICK:
+                nc.vector.quantize_mx(out=mem_c[:].bitcast(FP8X4), scales=mem_s[:], in_=mem_g[:])
+            if tick % 2 == 1 and 0 <= (tick - 3) // 2 <= 7:
+                v_recip((tick - 3) // 2)
+            if tick % 2 == 0 and 0 <= (tick - 8) // 2 <= 5:
+                v_qr((tick - 8) // 2)
+            if tick in (22, 24):
+                v_qr(tick // 2 - 5)
+            if tick in QW_TICK:
+                v_qw(*QW_TICK[tick])
+            for g, piece in V_FILL.get(tick, []):
+                regroup_w("v", g, 0, piece, 4)
+            if tick == NT:
+                big = keep.tile([P, NT * P * 4], BF16, name="w_g1", tag="big", align_bytes=64)
+                w_g[0, 1] = big[:, 0 : 4 * HALF]
+                w_g[1, 1] = big[:, 4 * HALF : 8 * HALF]
+                for g in range(2):
+                    for piece in range(4):
+                        regroup_w("g", g, 1, piece, 4)
+
+            if tick < NT:
+                i = tick
+                woven = []
+                if tick % 2 == 0 and 2 <= (tick + 2) // 2 <= 7:
+                    woven += [(pe_xt, (tick + 2) // 2, w) for w in range(4)]
+                if tick % 2 == 0 and 0 <= (tick - 4) // 2:
+                    woven += [(pe_rt, (tick - 4) // 2, a) for a in range(2)]
+                if tick % 2 == 1 and tick >= 3:
+                    woven += [(pe_et, (tick - 3) // 2, w) for w in range(8)]
+                slots = [0, 2] if tick >= 6 else [0, 1, 2]
+                per = -(-len(woven) // len(slots))
+                en = bank(i % 2, [P, SLOTS], F32)
+                for t in range(4):
+                    if t == 1 and tick >= 6:
+                        pe_m2(tick - 6)
+                        v_rg(tick - 6)
+                    if t in slots:
+                        for fn, k, w in woven[per * slots.index(t) : per * slots.index(t) + per]:
+                            fn(k, w)
+                    u, e = divmod(t, 2)
+                    nc.tensor.matmul(
+                        out=en[:], lhsT=x_gb[:, i, :, t], rhs=mem_tb[:, u, :, e], start=(t == 0), stop=(t == 3)
+                    )
+                if tick % 2 == 0 and 2 <= (tick + 2) // 2 <= 7:
+                    evac_xt(nc.scalar.copy, (tick + 2) // 2)
+                if tick % 2 == 0 and 0 <= (tick - 4) // 2:
+                    s_evac_rt((tick - 4) // 2)
+                if tick % 2 == 1 and 0 <= (tick - 5) // 2:
+                    v_qe((tick - 5) // 2)
+                nc.vector.tensor_reduce(out=negmax[:, i : i + 1], in_=en[:], axis=AX.X, op=ALU.max, negate=True)
+                e_sb[i] = ring.tile([P, SLOTS], BF16, name="e_sb", bufs=6)
+                nc.scalar.activation(
+                    out=e_sb[i][:],
+                    in_=en[:],
+                    func=ACT.Exp,
+                    bias=negmax[:, i : i + 1],
+                    scale=1.0,
+                    accum_out=rowsum[:, i : i + 1],
+                )
+            else:
+                if tick == BUNCH:
+                    for a in range(2):
+                        pe_rt(6, a)
+                        pe_rt(7, a)
+                    for w in range(8):
+                        pe_et(7, w)
+                    s_evac_rt(6)
+                    s_evac_rt(7)
+                    s_evac_et(7)
+                late = {16: 10, 17: 11, 20: 12, 21: 13, 22: 14, 23: 15}.get(tick)
+                if late is not None:
+                    pe_m2(late)
+                banks = [0, 1, 2] + ([3, 4, 5] if tick >= 20 else []) + ([6, 7] if tick >= 25 else [])
+                m3(units[tick - NT][0], units[tick - NT][1], banks, tick == NT + len(units) - 1)
+                if late is not None:
+                    v_rg(late)
+                if tick % 2 == 1 and (tick - 5) // 2 <= 7:
+                    v_qe((tick - 5) // 2)

@@ -92,10 +92,15 @@ def tile_dynamicmemorybank_pa_kernel(tc, x, memory, w1, b1, out):
                 out=x_sb[g][:].rearrange("p (i c) -> p i c", i=4), in_=x_v[:, 4 * g : 4 * g + 4, :]
             )
 
-        nc.sync.dma_start(out=mem_sb[:].rearrange("p (j c) -> p j c", j=4), in_=mem_v)
-        load_x(0)
+        mem_d = mem_sb[:].rearrange("p (j c) -> p j c", j=4)
+        x0_d = x_sb[0][:].rearrange("p (i c) -> p i c", i=4)
+        for u in range(2):
+            nc.sync.dma_start(out=mem_d[:, :, 256 * u : 256 * u + 256], in_=mem_v[:, :, 256 * u : 256 * u + 256])
+            nc.sync.dma_start(out=x0_d[:, 2 * u : 2 * u + 2, :], in_=x_v[:, 2 * u : 2 * u + 2, :])
+        x1_d = x_sb[1][:].rearrange("p (i c) -> p i c", i=4)
+        nc.sync.dma_start(out=x1_d[:, 0:2, :], in_=x_v[:, 4:6, :])
         load_w(0, 0)
-        load_x(1)
+        nc.sync.dma_start(out=x1_d[:, 2:4, :], in_=x_v[:, 6:8, :])
         load_w(1, 0)
         load_x(2)
         load_w(0, 1)
@@ -224,7 +229,7 @@ def tile_dynamicmemorybank_pa_kernel(tc, x, memory, w1, b1, out):
         acc_count = [0]
 
         def m3(h, i, banks, split):
-            v = ring.tile([P, HALF], F32, name="v", bufs=6)
+            v = ring.tile([P, HALF], F32, name="v", bufs=10)
             for fc in range(2):
                 acc = bank(banks[acc_count[0] % len(banks)], [P, 512], F32)
                 acc_count[0] += 1
@@ -268,29 +273,20 @@ def tile_dynamicmemorybank_pa_kernel(tc, x, memory, w1, b1, out):
             mt = bank(u, [P, 4, P], F32)
             for j in range(4):
                 nc.tensor.transpose(mt[:, j, :], mem_w[:, j, P * u : P * u + P], ident_f[:])
-            dst = mem_t[:, SLOTS * u : SLOTS * u + SLOTS]
-            if u == 0:
-                nc.scalar.copy(out=dst, in_=mt[:].rearrange("p j r -> p (j r)"))
-            else:
-                nc.vector.tensor_copy(out=dst, in_=mt[:].rearrange("p j r -> p (j r)"))
-        nc.gpsimd.tensor_scalar(
-            out=mem_g[:].rearrange("p (q m j) -> p q m j", q=4, m=P, j=4),
-            in0=mem_sb[:].rearrange("p (j m q) -> p q m j", j=4, m=P, q=4),
-            scalar1=1.0,
-            scalar2=0.0,
-            op0=ALU.mult,
-            op1=ALU.add,
-        )
-        for k in range(2):
+            nc.scalar.copy(out=mem_t[:, SLOTS * u : SLOTS * u + SLOTS], in_=mt[:].rearrange("p j r -> p (j r)"))
             for which in range(4):
-                pe_xt(k, which, 2 + k)
-            evac_xt(nc.scalar.copy if k == 0 else nc.vector.tensor_copy, k)
+                pe_xt(u, which, 2 + u)
+            evac_xt(nc.scalar.copy, u)
+        nc.vector.tensor_copy(
+            out=mem_g[:].rearrange("p (q m j) -> p q m j", q=4, m=P, j=4),
+            in_=mem_sb[:].rearrange("p (j m q) -> p q m j", j=4, m=P, q=4),
+        )
+        nc.vector.quantize_mx(out=mem_c[:].bitcast(FP8X4), scales=mem_s[:], in_=mem_g[:])
 
-        V_FILL = {3: [(1, 0)], 4: [(1, 1)]}
-        S_FILL = {3: [(1, 2)], 5: [(1, 3)]}
-        QW_TICK = {7: (0, 0), 9: (1, 0), 22: (0, 1), 27: (1, 1)}
-        QX_TICK = {5: 0, 6: 1, 10: 2, 14: 3}
-        QMEM_TICK = 5
+        V_FILL = {4: [(1, 0)], 5: [(1, 1)]}
+        S_FILL = {5: [(1, 2)], 7: [(1, 3)]}
+        QW_TICK = {7: (0, 0), 10: (1, 0), 22: (0, 1), 27: (1, 1)}
+        QX_TICK = {1: 0, 6: 1, 10: 2, 14: 3}
         for piece in range(4):
             regroup_w("g", 0, 0, piece, 4)
         BUNCH = 18
@@ -304,8 +300,6 @@ def tile_dynamicmemorybank_pa_kernel(tc, x, memory, w1, b1, out):
                 regroup_w("s", g, 0, piece, 4)
             if tick in QX_TICK:
                 v_qx(QX_TICK[tick])
-            if tick == QMEM_TICK:
-                nc.vector.quantize_mx(out=mem_c[:].bitcast(FP8X4), scales=mem_s[:], in_=mem_g[:])
             if tick % 2 == 1 and 0 <= (tick - 3) // 2 <= 7:
                 v_recip((tick - 3) // 2)
             if tick % 2 == 0 and 0 <= (tick - 8) // 2 <= 5:

@@ -92,15 +92,10 @@ def tile_dynamicmemorybank_pa_kernel(tc, x, memory, w1, b1, out):
                 out=x_sb[g][:].rearrange("p (i c) -> p i c", i=4), in_=x_v[:, 4 * g : 4 * g + 4, :]
             )
 
-        mem_d = mem_sb[:].rearrange("p (j c) -> p j c", j=4)
-        x0_d = x_sb[0][:].rearrange("p (i c) -> p i c", i=4)
-        for u in range(2):
-            nc.sync.dma_start(out=mem_d[:, :, 256 * u : 256 * u + 256], in_=mem_v[:, :, 256 * u : 256 * u + 256])
-            nc.sync.dma_start(out=x0_d[:, 2 * u : 2 * u + 2, :], in_=x_v[:, 2 * u : 2 * u + 2, :])
-        x1_d = x_sb[1][:].rearrange("p (i c) -> p i c", i=4)
-        nc.sync.dma_start(out=x1_d[:, 0:2, :], in_=x_v[:, 4:6, :])
+        nc.sync.dma_start(out=mem_sb[:].rearrange("p (j c) -> p j c", j=4), in_=mem_v)
+        load_x(0)
         load_w(0, 0)
-        nc.sync.dma_start(out=x1_d[:, 2:4, :], in_=x_v[:, 6:8, :])
+        load_x(1)
         load_w(1, 0)
         load_x(2)
         load_w(0, 1)
@@ -229,7 +224,7 @@ def tile_dynamicmemorybank_pa_kernel(tc, x, memory, w1, b1, out):
         acc_count = [0]
 
         def m3(h, i, banks, split):
-            v = ring.tile([P, HALF], F32, name="v", bufs=10)
+            v = ring.tile([P, HALF], F32, name="v", bufs=6)
             for fc in range(2):
                 acc = bank(banks[acc_count[0] % len(banks)], [P, 512], F32)
                 acc_count[0] += 1
@@ -273,22 +268,31 @@ def tile_dynamicmemorybank_pa_kernel(tc, x, memory, w1, b1, out):
             mt = bank(u, [P, 4, P], F32)
             for j in range(4):
                 nc.tensor.transpose(mt[:, j, :], mem_w[:, j, P * u : P * u + P], ident_f[:])
-            nc.scalar.copy(out=mem_t[:, SLOTS * u : SLOTS * u + SLOTS], in_=mt[:].rearrange("p j r -> p (j r)"))
-            for which in range(4):
-                pe_xt(u, which, 2 + u)
-            evac_xt(nc.scalar.copy, u)
-        nc.vector.tensor_copy(
+            dst = mem_t[:, SLOTS * u : SLOTS * u + SLOTS]
+            if u == 0:
+                nc.scalar.copy(out=dst, in_=mt[:].rearrange("p j r -> p (j r)"))
+            else:
+                nc.vector.tensor_copy(out=dst, in_=mt[:].rearrange("p j r -> p (j r)"))
+        nc.gpsimd.tensor_scalar(
             out=mem_g[:].rearrange("p (q m j) -> p q m j", q=4, m=P, j=4),
-            in_=mem_sb[:].rearrange("p (j m q) -> p q m j", j=4, m=P, q=4),
+            in0=mem_sb[:].rearrange("p (j m q) -> p q m j", j=4, m=P, q=4),
+            scalar1=1.0,
+            scalar2=0.0,
+            op0=ALU.mult,
+            op1=ALU.add,
         )
-        nc.vector.quantize_mx(out=mem_c[:].bitcast(FP8X4), scales=mem_s[:], in_=mem_g[:])
+        for k in range(2):
+            for which in range(4):
+                pe_xt(k, which, 2 + k)
+            evac_xt(nc.scalar.copy if k == 0 else nc.vector.tensor_copy, k)
 
-        V_FILL = {4: [(1, 0)], 5: [(1, 1)]}
-        S_FILL = {5: [(1, 2)], 7: [(1, 3)]}
-        QW_TICK = {7: (0, 0), 10: (1, 0), 22: (0, 1), 27: (1, 1)}
-        QX_TICK = {1: 0, 6: 1, 10: 2, 14: 3}
-        for piece in range(4):
-            regroup_w("g", 0, 0, piece, 4)
+        V_FILL = {3: [(1, 0)], 4: [(1, 1)]}
+        S_FILL = {3: [(1, 2)], 5: [(1, 3)]}
+        QW_TICK = {7: (0, 0), 9: (1, 0), 22: (0, 1), 27: (1, 1)}
+        QX_TICK = {5: 0, 6: 1, 10: 2, 14: 3}
+        QMEM_TICK = 5
+        for piece in range(16):
+            regroup_w("g", 0, 0, piece, 16)
         BUNCH = 18
         units = [(h, i) for h in range(2) for i in range(NT)]
         for tick in range(NT + len(units)):
@@ -300,6 +304,8 @@ def tile_dynamicmemorybank_pa_kernel(tc, x, memory, w1, b1, out):
                 regroup_w("s", g, 0, piece, 4)
             if tick in QX_TICK:
                 v_qx(QX_TICK[tick])
+            if tick == QMEM_TICK:
+                nc.vector.quantize_mx(out=mem_c[:].bitcast(FP8X4), scales=mem_s[:], in_=mem_g[:])
             if tick % 2 == 1 and 0 <= (tick - 3) // 2 <= 7:
                 v_recip((tick - 3) // 2)
             if tick % 2 == 0 and 0 <= (tick - 8) // 2 <= 5:
@@ -315,8 +321,8 @@ def tile_dynamicmemorybank_pa_kernel(tc, x, memory, w1, b1, out):
                 w_g[0, 1] = big[:, 0 : 4 * HALF]
                 w_g[1, 1] = big[:, 4 * HALF : 8 * HALF]
                 for g in range(2):
-                    for piece in range(4):
-                        regroup_w("g", g, 1, piece, 4)
+                    for piece in range(16):
+                        regroup_w("g", g, 1, piece, 16)
 
             if tick < NT:
                 i = tick

@@ -18,9 +18,29 @@ C = 512
 SLOTS = 512
 F = 2048
 NT = TOKENS // P
+NPAIR = NT // 2
 HALF = F // 2
+BANK = 512
 FLOPS = 2 * TOKENS * C * SLOTS * 2 + 2 * TOKENS * 2 * C * F
-PIN = True
+
+EN_BANKS = (0, 1)
+XT_BANK = 2
+ET_BANKS = (3, 4)
+RT_BANK = 5
+M2_BANKS = (6, 7)
+
+XT_AT = -2
+ET_AT = 3
+RT_AT = 4
+M2_AT = 6
+ATTENTION_DONE = NT + M2_AT
+
+W_PIECE = 256
+
+
+def pair_due(tick, offset, first=0):
+    k, odd = divmod(tick - offset, 2)
+    return k if odd == 0 and first <= k < NPAIR else None
 
 
 def tile_dynamicmemorybank_pa_kernel(tc, x, memory, w1, b1, out):
@@ -29,18 +49,17 @@ def tile_dynamicmemorybank_pa_kernel(tc, x, memory, w1, b1, out):
         keep = ctx.enter_context(tc.tile_pool(name="keep", bufs=1))
         ring = ctx.enter_context(tc.tile_pool(name="ring", bufs=2))
         psum = ctx.enter_context(tc.psum_pool(name="psum", bufs=1))
-        if PIN:
-            ctx.enter_context(tc.manual_schedule())
+        ctx.enter_context(tc.manual_schedule())
 
         x_v = x.flatten_outer_dims().rearrange("(p i) c -> p i c", i=NT)
         out_v = out.flatten_outer_dims().rearrange("(p i) f -> p i f", i=NT)
         mem_v = memory.flatten_outer_dims().rearrange("(p j) c -> p j c", j=4)
 
-        count = [0]
+        made = [0]
 
         def bank(k, shape, dtype):
-            count[0] += 1
-            return psum.tile(shape, dtype, tag="bank%d" % k, name="ps%d" % count[0])
+            made[0] += 1
+            return psum.tile(shape, dtype, tag="bank%d" % k, name="ps%d" % made[0])
 
         ident_f = keep.tile([P, P], F32, name="ident_f")
         ident_b = keep.tile([P, P], BF16, name="ident_b")
@@ -53,7 +72,7 @@ def tile_dynamicmemorybank_pa_kernel(tc, x, memory, w1, b1, out):
         mem_c = keep.tile([P, C], U32, name="mem_c", align_bytes=64)
         mem_s = keep.tile([P, C], U8, name="mem_s", align_bytes=64)
         x_sb = [keep.tile([P, 4 * C], BF16, name="x_sb%d" % g) for g in range(4)]
-        x_g = keep.tile([P, NT * P * 4], BF16, name="x_g", tag="big", align_bytes=64)
+        x_g = keep.tile([P, NT * P * 4], BF16, name="x_g", align_bytes=64)
         x_c = keep.tile([P, TOKENS], U32, name="x_c", align_bytes=64)
         x_s = keep.tile([P, TOKENS], U8, name="x_s", align_bytes=64)
         r_c = keep.tile([P, TOKENS], U32, name="r_c", align_bytes=64)
@@ -62,22 +81,31 @@ def tile_dynamicmemorybank_pa_kernel(tc, x, memory, w1, b1, out):
         rowsum = keep.tile([P, NT], F32, name="rowsum")
         recip = keep.tile([P, NT], F32, name="recip")
         bias = keep.tile([P, F], BF16, name="bias")
-        w_raw = {}
+        warm = keep.tile([P, 2], F32, name="warm")
+        w_sb = {}
+        w_g = {}
         w_c = {}
         w_s = {}
         for h in range(2):
             for g in range(2):
-                w_raw[g, h] = keep.tile([P, 4 * HALF], BF16, name="w_raw%d%d" % (g, h))
+                w_sb[g, h] = keep.tile([P, 4 * HALF], BF16, name="w_sb%d%d" % (g, h))
+                w_g[g, h] = keep.tile([P, 4 * HALF], BF16, name="w_g%d%d" % (g, h), align_bytes=64)
                 w_c[g, h] = keep.tile([P, HALF], U32, name="w_c%d%d" % (g, h), align_bytes=64)
                 w_s[g, h] = keep.tile([P, HALF], U8, name="w_s%d%d" % (g, h), align_bytes=64)
 
-        x_gw = x_g[:].bitcast(F32).rearrange("p (i r u) -> p i r u", i=NT, r=P, u=2)
-        x_gb = x_g[:].rearrange("p (i r t) -> p i r t", i=NT, r=P, t=4)
-        mem_tb = mem_t[:].bitcast(BF16).rearrange("p (u c e) -> p u c e", u=2, e=2)
+        x_words = x_g[:].bitcast(F32).rearrange("p (i r u) -> p i r u", i=NT, r=P, u=2)
+        x_values = x_g[:].rearrange("p (i r t) -> p i r t", i=NT, r=P, t=4)
+        mem_values = mem_t[:].bitcast(BF16).rearrange("p (u c e) -> p u c e", u=2, e=2)
+        mem_words = mem_sb[:].bitcast(F32).rearrange("p (j w) -> p j w", j=4)
+
+        def load_x(g):
+            nc.sync.dma_start(
+                out=x_sb[g][:].rearrange("p (i c) -> p i c", i=4), in_=x_v[:, 4 * g : 4 * g + 4, :]
+            )
 
         def load_w(g, h):
             cols = slice(h * HALF, (h + 1) * HALF)
-            dst = w_raw[g, h][:].rearrange("p (t f) -> p t f", t=4)
+            dst = w_sb[g, h][:].rearrange("p (t f) -> p t f", t=4)
             if g == 0:
                 for u in range(2):
                     nc.sync.dma_start(
@@ -87,20 +115,10 @@ def tile_dynamicmemorybank_pa_kernel(tc, x, memory, w1, b1, out):
             else:
                 nc.sync.dma_start(out=dst, in_=w1[C : 2 * C, cols].rearrange("(p j) f -> p j f", j=4))
 
-        def load_x(g):
-            nc.sync.dma_start(
-                out=x_sb[g][:].rearrange("p (i c) -> p i c", i=4), in_=x_v[:, 4 * g : 4 * g + 4, :]
-            )
-
         nc.sync.dma_start(out=mem_sb[:].rearrange("p (j c) -> p j c", j=4), in_=mem_v)
-        load_x(0)
-        load_w(0, 0)
-        load_x(1)
-        load_w(1, 0)
-        load_x(2)
-        load_w(0, 1)
-        load_x(3)
-        load_w(1, 1)
+        for n in range(4):
+            load_x(n)
+            load_w(n % 2, n // 2)
         nc.sync.dma_start(out=bias[:], in_=b1.partition_broadcast(P))
 
         xt_ps = {}
@@ -114,57 +132,74 @@ def tile_dynamicmemorybank_pa_kernel(tc, x, memory, w1, b1, out):
         r_g = {}
         m2_ps = {}
 
-        def pe_xt(k, which, b=2):
-            if which == 0:
-                xt_ps[k] = bank(b, [P, 2, 2, P], F32)
-            a, u = divmod(which, 2)
-            i = 2 * k + a
-            src = x_sb[i // 4][:].bitcast(F32).rearrange("p (i w) -> p i w", i=4)
-            nc.tensor.transpose(xt_ps[k][:, a, u, :], src[:, i % 4, P * u : P * u + P], ident_f[:])
+        def x_transposes(k, b):
+            xt_ps[k] = bank(b, [P, 2, 2, P], F32)
+            calls = []
+            for a in range(2):
+                i = 2 * k + a
+                words = x_sb[i // 4][:].bitcast(F32).rearrange("p (i w) -> p i w", i=4)
+                for u in range(2):
+                    calls.append((xt_ps[k][:, a, u, :], words[:, i % 4, P * u : P * u + P], ident_f[:]))
+            return calls
 
-        def evac_xt(eng_copy, k):
-            eng_copy(out=x_gw[:, 2 * k : 2 * k + 2, :, :], in_=xt_ps[k][:].rearrange("p a u r -> p a r u"))
+        def x_copy_out(copy, k):
+            copy(out=x_words[:, 2 * k : 2 * k + 2, :, :], in_=xt_ps[k][:].rearrange("p a u r -> p a r u"))
 
-        def v_qx(g):
-            cols = slice(512 * g, 512 * g + 512)
+        def x_quantise(g):
+            cols = slice(4 * P * g, 4 * P * (g + 1))
             nc.vector.quantize_mx(
-                out=x_c[:, cols].bitcast(FP8X4), scales=x_s[:, cols], in_=x_g[:, 2048 * g : 2048 * g + 2048]
+                out=x_c[:, cols].bitcast(FP8X4), scales=x_s[:, cols], in_=x_g[:, 16 * P * g : 16 * P * (g + 1)]
             )
 
-        def pe_et(k, which):
-            if which == 0:
-                et_ps[k] = bank(3 + k % 2, [P, 2, 4, P], BF16)
-            a, t = divmod(which, 4)
-            nc.tensor.transpose(et_ps[k][:, a, t, :], e_sb[2 * k + a][:, P * t : P * t + P], ident_b[:])
+        def energy_softmax_tail(i, en):
+            nc.vector.tensor_reduce(out=negmax[:, i : i + 1], in_=en[:], axis=AX.X, op=ALU.max, negate=True)
+            e_sb[i] = ring.tile([P, SLOTS], BF16, name="e_sb", bufs=6)
+            nc.scalar.activation(
+                out=e_sb[i][:],
+                in_=en[:],
+                func=ACT.Exp,
+                bias=negmax[:, i : i + 1],
+                scale=1.0,
+                accum_out=rowsum[:, i : i + 1],
+            )
 
-        def s_evac_et(k):
+        def e_transposes(k):
+            et_ps[k] = bank(ET_BANKS[k % 2], [P, 2, 4, P], BF16)
+            return [
+                (et_ps[k][:, a, t, :], e_sb[2 * k + a][:, P * t : P * t + P], ident_b[:])
+                for a in range(2)
+                for t in range(4)
+            ]
+
+        def e_copy_out(k):
             e_g[k] = ring.tile([P, 2 * P * 4], BF16, name="e_g", align_bytes=64)
             nc.scalar.copy(
                 out=e_g[k][:].rearrange("p (a r t) -> p a r t", a=2, r=P, t=4),
                 in_=et_ps[k][:].rearrange("p a t r -> p a r t"),
             )
 
-        def v_qe(k):
+        def e_quantise(k):
             e_c[k] = ring.tile([P, 2 * P], U32, name="e_c", align_bytes=64)
             e_s[k] = ring.tile([P, 2 * P], U8, name="e_s", align_bytes=64)
             nc.vector.quantize_mx(out=e_c[k][:].bitcast(FP8X4), scales=e_s[k][:], in_=e_g[k][:])
 
-        def v_recip(k):
+        def reciprocals(k):
             nc.vector.reciprocal(out=recip[:, 2 * k : 2 * k + 2], in_=rowsum[:, 2 * k : 2 * k + 2])
 
-        def pe_rt(k, a):
-            if a == 0:
-                rt_ps[k] = bank(3 if k == 7 else 5, [P, 2, P], F32)
-            i = 2 * k + a
-            nc.tensor.transpose(rt_ps[k][:, a, :], recip[:, i : i + 1].to_broadcast([P, P]), ident_f[:])
+        def recip_transposes(k):
+            rt_ps[k] = bank(RT_BANK, [P, 2, P], F32)
+            return [
+                (rt_ps[k][:, a, :], recip[:, 2 * k + a : 2 * k + a + 1].to_broadcast([P, P]), ident_f[:])
+                for a in range(2)
+            ]
 
-        def s_evac_rt(k):
+        def recip_copy_out(k):
             r_b[k] = ring.tile([P, 2, P], F32, name="r_b", bufs=3)
             nc.scalar.copy(out=r_b[k][:], in_=rt_ps[k][:])
 
-        def pe_m2(i):
+        def retrieve(i):
             k, a = divmod(i, 2)
-            m2_ps[i] = bank(6 + i % 2, [P, 4, P], F32)
+            m2_ps[i] = bank(M2_BANKS[a], [P, 4, P], F32)
             for q in range(4):
                 nc.tensor.matmul_mx(
                     out=m2_ps[i][:, q, :],
@@ -176,209 +211,153 @@ def tile_dynamicmemorybank_pa_kernel(tc, x, memory, w1, b1, out):
                     stop=True,
                 )
 
-        def v_rg(i):
+        def normalise(i):
             k, a = divmod(i, 2)
             if a == 0:
                 r_g[k] = ring.tile([P, 2 * P * 4], BF16, name="r_g", align_bytes=64)
-            dst = r_g[k][:].rearrange("p (a r q) -> p a r q", a=2, r=P, q=4)
             nc.vector.tensor_tensor(
-                out=dst[:, a, :, :],
+                out=r_g[k][:].rearrange("p (a r q) -> p a r q", a=2, r=P, q=4)[:, a, :, :],
                 in0=m2_ps[i][:].rearrange("p q r -> p r q"),
                 in1=r_b[k][:, a, :].unsqueeze(2).to_broadcast([P, P, 4]),
                 op=ALU.mult,
             )
 
-        def v_qr(k):
-            cols = slice(256 * k, 256 * k + 256)
+        def r_quantise(k):
+            cols = slice(2 * P * k, 2 * P * (k + 1))
             nc.vector.quantize_mx(out=r_c[:, cols].bitcast(FP8X4), scales=r_s[:, cols], in_=r_g[k][:])
 
-        w_g = {}
-        w_g00 = keep.tile([P, 4 * HALF], BF16, name="w_g00", align_bytes=64)
-        w_g10 = keep.tile([P, 4 * HALF], BF16, name="w_g10", align_bytes=64)
-        w_g[0, 0] = w_g00[:]
-        w_g[1, 0] = w_g10[:]
+        def mem_regroup():
+            nc.vector.tensor_copy(
+                out=mem_g[:].rearrange("p (q m j) -> p q m j", q=4, m=P, j=4),
+                in_=mem_sb[:].rearrange("p (j m q) -> p q m j", j=4, m=P, q=4),
+            )
 
-        def regroup_w(eng, g, h, piece, pieces):
-            n = HALF // pieces
-            cols = slice(n * piece, n * piece + n)
-            if eng == "g":
-                nc.gpsimd.tensor_scalar(
-                    out=w_g[g, h].rearrange("p (f t) -> p f t", t=4)[:, cols, :],
-                    in0=w_raw[g, h][:].rearrange("p (t f) -> p f t", t=4)[:, cols, :],
-                    scalar1=1.0,
-                    scalar2=0.0,
-                    op0=ALU.mult,
-                    op1=ALU.add,
-                )
-            else:
-                dst = w_g[g, h].rearrange("p (f t) -> p f t", t=4)[:, cols, :].rearrange("p (c i) t -> p c t i", i=4)
-                src = w_raw[g, h][:].rearrange("p (t f) -> p t f", t=4)[:, :, cols].rearrange("p t (c i) -> p c t i", i=4)
-                if eng == "v":
-                    nc.vector.tensor_copy(out=dst, in_=src)
-                else:
-                    nc.scalar.copy(out=dst, in_=src)
+        def w_regroup(copy, g, h, piece):
+            cols = slice(W_PIECE * piece, W_PIECE * (piece + 1))
+            copy(
+                out=w_g[g, h][:].rearrange("p (f t) -> p f t", t=4)[:, cols, :].rearrange("p (c i) t -> p c t i", i=4),
+                in_=w_sb[g, h][:].rearrange("p (t f) -> p t f", t=4)[:, :, cols].rearrange("p t (c i) -> p c t i", i=4),
+            )
 
-        def v_qw(g, h):
-            nc.vector.quantize_mx(out=w_c[g, h][:].bitcast(FP8X4), scales=w_s[g, h][:], in_=w_g[g, h])
+        def w_quantise(g, h):
+            nc.vector.quantize_mx(out=w_c[g, h][:].bitcast(FP8X4), scales=w_s[g, h][:], in_=w_g[g, h][:])
 
-        acc_count = [0]
+        used = [0]
 
-        def m3(h, i, banks, split):
+        def fuse(h, i, banks, stores):
             v = ring.tile([P, HALF], F32, name="v", bufs=6)
-            for fc in range(2):
-                acc = bank(banks[acc_count[0] % len(banks)], [P, 512], F32)
-                acc_count[0] += 1
-                cols = slice(512 * fc, 512 * fc + 512)
-                toks = slice(P * i, P * i + P)
-                nc.tensor.matmul_mx(
-                    out=acc[:],
-                    lhsT=x_c[:, toks].bitcast(FP8X4),
-                    lhsT_scale=x_s[:, toks],
-                    rhs=w_c[0, h][:, cols].bitcast(FP8X4),
-                    rhs_scale=w_s[0, h][:, cols],
-                    start=True,
-                    stop=False,
-                )
-                nc.tensor.matmul_mx(
-                    out=acc[:],
-                    lhsT=r_c[:, toks].bitcast(FP8X4),
-                    lhsT_scale=r_s[:, toks],
-                    rhs=w_c[1, h][:, cols].bitcast(FP8X4),
-                    rhs_scale=w_s[1, h][:, cols],
-                    start=False,
-                    stop=True,
-                )
-                nc.vector.tensor_tensor(
-                    out=v[:, cols], in0=acc[:], in1=bias[:, h * HALF + 512 * fc : h * HALF + 512 * fc + 512], op=ALU.add
-                )
-                if split:
-                    nc.scalar.activation(out=v[:, cols], in_=v[:, cols], func=ACT.Silu)
-                    nc.sync.dma_start(
-                        out=out_v[:, i, h * HALF + 512 * fc : h * HALF + 512 * fc + 512], in_=v[:, cols]
+            toks = slice(P * i, P * (i + 1))
+            for fc in range(HALF // BANK):
+                acc = bank(banks[used[0] % len(banks)], [P, BANK], F32)
+                used[0] += 1
+                lo, hi = BANK * fc, BANK * (fc + 1)
+                cols = slice(lo, hi)
+                for g, codes, scales in ((0, x_c, x_s), (1, r_c, r_s)):
+                    nc.tensor.matmul_mx(
+                        out=acc[:],
+                        lhsT=codes[:, toks].bitcast(FP8X4),
+                        lhsT_scale=scales[:, toks],
+                        rhs=w_c[g, h][:, cols].bitcast(FP8X4),
+                        rhs_scale=w_s[g, h][:, cols],
+                        start=(g == 0),
+                        stop=(g == 1),
                     )
-            if not split:
-                nc.scalar.activation(out=v[:], in_=v[:], func=ACT.Silu)
-                nc.sync.dma_start(out=out_v[:, i, h * HALF : (h + 1) * HALF], in_=v[:])
+                nc.vector.tensor_tensor(
+                    out=v[:, cols], in0=acc[:], in1=bias[:, h * HALF + lo : h * HALF + hi], op=ALU.add
+                )
+                if stores == 2 or hi == HALF:
+                    lo = lo if stores == 2 else 0
+                    nc.scalar.activation(out=v[:, lo:hi], in_=v[:, lo:hi], func=ACT.Silu)
+                    nc.sync.dma_start(out=out_v[:, i, h * HALF + lo : h * HALF + hi], in_=v[:, lo:hi])
 
-        warm = keep.tile([P, 2], F32, name="warm")
         nc.vector.memset(warm[:], 0.0)
         nc.scalar.activation(out=warm[:, 0:1], in_=warm[:, 1:2], func=ACT.Exp)
-        mem_w = mem_sb[:].bitcast(F32).rearrange("p (j w) -> p j w", j=4)
         for u in range(2):
-            mt = bank(u, [P, 4, P], F32)
+            mt = bank(EN_BANKS[u], [P, 4, P], F32)
             for j in range(4):
-                nc.tensor.transpose(mt[:, j, :], mem_w[:, j, P * u : P * u + P], ident_f[:])
-            dst = mem_t[:, SLOTS * u : SLOTS * u + SLOTS]
-            if u == 0:
-                nc.scalar.copy(out=dst, in_=mt[:].rearrange("p j r -> p (j r)"))
-            else:
-                nc.vector.tensor_copy(out=dst, in_=mt[:].rearrange("p j r -> p (j r)"))
-        nc.gpsimd.tensor_scalar(
-            out=mem_g[:].rearrange("p (q m j) -> p q m j", q=4, m=P, j=4),
-            in0=mem_sb[:].rearrange("p (j m q) -> p q m j", j=4, m=P, q=4),
-            scalar1=1.0,
-            scalar2=0.0,
-            op0=ALU.mult,
-            op1=ALU.add,
-        )
+                nc.tensor.transpose(mt[:, j, :], mem_words[:, j, P * u : P * u + P], ident_f[:])
+            copy = nc.scalar.copy if u == 0 else nc.vector.tensor_copy
+            copy(out=mem_t[:, SLOTS * u : SLOTS * (u + 1)], in_=mt[:].rearrange("p j r -> p (j r)"))
         for k in range(2):
-            for which in range(4):
-                pe_xt(k, which, 2 + k)
-            evac_xt(nc.scalar.copy if k == 0 else nc.vector.tensor_copy, k)
+            for call in x_transposes(k, XT_BANK + k):
+                nc.tensor.transpose(*call)
+            x_copy_out(nc.scalar.copy if k == 0 else nc.vector.tensor_copy, k)
 
-        V_FILL = {3: [(1, 0)], 4: [(1, 1)]}
-        S_FILL = {3: [(1, 2)], 5: [(1, 3)]}
-        QW_TICK = {7: (0, 0), 9: (1, 0), 22: (0, 1), 27: (1, 1)}
-        QX_TICK = {5: 0, 6: 1, 10: 2, 14: 3}
-        QMEM_TICK = 5
-        for piece in range(16):
-            regroup_w("g", 0, 0, piece, 16)
-        BUNCH = 18
-        units = [(h, i) for h in range(2) for i in range(NT)]
-        for tick in range(NT + len(units)):
-            if tick % 2 == 0 and 0 <= (tick - 4) // 2 <= 6:
-                s_evac_et((tick - 4) // 2)
+        last_tick = NT + 2 * NT - 1
+        for tick in range(last_tick + 1):
+            energy_tick = tick < NT
+            xt = pair_due(tick, XT_AT, 2)
+            et = pair_due(tick, ET_AT)
+            rt = pair_due(tick, RT_AT)
+            m2 = tick - M2_AT if 0 <= tick - M2_AT < NT else None
+
+            if pair_due(tick, ET_AT + 1) is not None:
+                e_copy_out(pair_due(tick, ET_AT + 1))
             if tick == NT:
                 nc.scalar.activation(out=warm[:, 0:1], in_=warm[:, 1:2], func=ACT.Silu)
-            for g, piece in S_FILL.get(tick, []):
-                regroup_w("s", g, 0, piece, 4)
-            if tick in QX_TICK:
-                v_qx(QX_TICK[tick])
-            if tick == QMEM_TICK:
-                nc.vector.quantize_mx(out=mem_c[:].bitcast(FP8X4), scales=mem_s[:], in_=mem_g[:])
-            if tick % 2 == 1 and 0 <= (tick - 3) // 2 <= 7:
-                v_recip((tick - 3) // 2)
-            if tick % 2 == 0 and 0 <= (tick - 8) // 2 <= 5:
-                v_qr((tick - 8) // 2)
-            if tick in (22, 24):
-                v_qr(tick // 2 - 5)
-            if tick in QW_TICK:
-                v_qw(*QW_TICK[tick])
-            for g, piece in V_FILL.get(tick, []):
-                regroup_w("v", g, 0, piece, 4)
-            if tick == NT:
-                big = keep.tile([P, NT * P * 4], BF16, name="w_g1", tag="big", align_bytes=64)
-                w_g[0, 1] = big[:, 0 : 4 * HALF]
-                w_g[1, 1] = big[:, 4 * HALF : 8 * HALF]
-                for g in range(2):
-                    for piece in range(16):
-                        regroup_w("g", g, 1, piece, 16)
+            if tick % 2 == 1 and 7 <= tick <= 21:
+                w_regroup(nc.scalar.copy, (tick - 7) // 8, 1, (tick - 7) // 2 % 4)
 
-            if tick < NT:
-                i = tick
-                woven = []
-                if tick % 2 == 0 and 2 <= (tick + 2) // 2 <= 7:
-                    woven += [(pe_xt, (tick + 2) // 2, w) for w in range(4)]
-                if tick % 2 == 0 and 0 <= (tick - 4) // 2:
-                    woven += [(pe_rt, (tick - 4) // 2, a) for a in range(2)]
-                if tick % 2 == 1 and tick >= 3:
-                    woven += [(pe_et, (tick - 3) // 2, w) for w in range(8)]
-                slots = [0, 2] if tick >= 6 else [0, 1, 2]
-                per = -(-len(woven) // len(slots))
-                en = bank(i % 2, [P, SLOTS], F32)
+            if tick % 4 == 2 and energy_tick:
+                x_quantise(tick // 4)
+            if tick == ET_AT + 2:
+                nc.vector.quantize_mx(out=mem_c[:].bitcast(FP8X4), scales=mem_s[:], in_=mem_g[:])
+            if pair_due(tick, RT_AT - 1) is not None:
+                reciprocals(pair_due(tick, RT_AT - 1))
+            if pair_due(tick, M2_AT + 2) is not None:
+                r_quantise(pair_due(tick, M2_AT + 2))
+            for g in range(2):
+                if tick == 4 * g + 7:
+                    w_quantise(g, 0)
+                if tick == 8 * g + 16:
+                    w_quantise(g, 1)
+            if tick == 0:
+                mem_regroup()
+            if 1 <= tick <= 8:
+                w_regroup(nc.vector.tensor_copy, (tick - 1) // 4, 0, (tick - 1) % 4)
+
+            transposes = []
+            if xt is not None:
+                transposes += x_transposes(xt, XT_BANK)
+            if rt is not None:
+                transposes += recip_transposes(rt)
+            if et is not None:
+                transposes += e_transposes(et)
+            if energy_tick:
+                first = (len(transposes) + 1) // 2
+                en = bank(EN_BANKS[tick % 2], [P, SLOTS], F32)
                 for t in range(4):
-                    if t == 1 and tick >= 6:
-                        pe_m2(tick - 6)
-                        v_rg(tick - 6)
-                    if t in slots:
-                        for fn, k, w in woven[per * slots.index(t) : per * slots.index(t) + per]:
-                            fn(k, w)
-                    u, e = divmod(t, 2)
+                    if t % 2 == 0:
+                        for call in transposes[:first] if t == 0 else transposes[first:]:
+                            nc.tensor.transpose(*call)
+                    if t == 1 and m2 is not None:
+                        retrieve(m2)
+                        normalise(m2)
                     nc.tensor.matmul(
-                        out=en[:], lhsT=x_gb[:, i, :, t], rhs=mem_tb[:, u, :, e], start=(t == 0), stop=(t == 3)
+                        out=en[:],
+                        lhsT=x_values[:, tick, :, t],
+                        rhs=mem_values[:, t // 2, :, t % 2],
+                        start=(t == 0),
+                        stop=(t == 3),
                     )
-                if tick % 2 == 0 and 2 <= (tick + 2) // 2 <= 7:
-                    evac_xt(nc.scalar.copy, (tick + 2) // 2)
-                if tick % 2 == 0 and 0 <= (tick - 4) // 2:
-                    s_evac_rt((tick - 4) // 2)
-                if tick % 2 == 1 and 0 <= (tick - 5) // 2:
-                    v_qe((tick - 5) // 2)
-                nc.vector.tensor_reduce(out=negmax[:, i : i + 1], in_=en[:], axis=AX.X, op=ALU.max, negate=True)
-                e_sb[i] = ring.tile([P, SLOTS], BF16, name="e_sb", bufs=6)
-                nc.scalar.activation(
-                    out=e_sb[i][:],
-                    in_=en[:],
-                    func=ACT.Exp,
-                    bias=negmax[:, i : i + 1],
-                    scale=1.0,
-                    accum_out=rowsum[:, i : i + 1],
-                )
             else:
-                if tick == BUNCH:
-                    for a in range(2):
-                        pe_rt(6, a)
-                        pe_rt(7, a)
-                    for w in range(8):
-                        pe_et(7, w)
-                    s_evac_rt(6)
-                    s_evac_rt(7)
-                    s_evac_et(7)
-                late = {16: 10, 17: 11, 20: 12, 21: 13, 22: 14, 23: 15}.get(tick)
-                if late is not None:
-                    pe_m2(late)
-                banks = [0, 1, 2] + ([3, 4, 5] if tick >= 20 else []) + ([6, 7] if tick >= 25 else [])
-                m3(units[tick - NT][0], units[tick - NT][1], banks, tick == NT + len(units) - 1)
-                if late is not None:
-                    v_rg(late)
-                if tick % 2 == 1 and (tick - 5) // 2 <= 7:
-                    v_qe((tick - 5) // 2)
+                for call in transposes:
+                    nc.tensor.transpose(*call)
+
+            if xt is not None:
+                x_copy_out(nc.scalar.copy, xt)
+            if rt is not None:
+                recip_copy_out(rt)
+
+            if not energy_tick:
+                banks = list(EN_BANKS) + [XT_BANK]
+                if tick >= ATTENTION_DONE:
+                    banks += list(ET_BANKS) + [RT_BANK] + list(M2_BANKS)
+                fuse((tick - NT) // NT, (tick - NT) % NT, banks, 2 if tick == last_tick else 1)
+                if m2 is not None:
+                    retrieve(m2)
+                    normalise(m2)
+            if pair_due(tick, ET_AT + 2) is not None:
+                e_quantise(pair_due(tick, ET_AT + 2))
+            if energy_tick:
+                energy_softmax_tail(tick, en)

@@ -23,16 +23,16 @@ HALF = F // 2
 BANK = 512
 FLOPS = 2 * TOKENS * C * SLOTS * 2 + 2 * TOKENS * 2 * C * F
 
-EN_BANKS = (0, 1)
-XT_BANK = 2
-ET_BANKS = (3, 4)
-RT_BANK = 5
-M2_BANKS = (6, 7)
+EN_BANKS = (0, 1, 2)
+XT_BANK = 3
+ET_BANKS = (4, 5)
+RT_BANK = 6
+M2_BANK = 7
 
 XT_AT = -2
 ET_AT = 3
 RT_AT = 4
-M2_AT = 6
+M2_AT = 7
 ATTENTION_DONE = NT + M2_AT
 
 W_PIECE = 256
@@ -199,7 +199,7 @@ def tile_dynamicmemorybank_pa_kernel(tc, x, memory, w1, b1, out):
 
         def retrieve(i):
             k, a = divmod(i, 2)
-            m2_ps[i] = bank(M2_BANKS[a], [P, 4, P], F32)
+            m2_ps[i] = bank(M2_BANK, [P, 4, P], F32)
             for q in range(4):
                 nc.tensor.matmul_mx(
                     out=m2_ps[i][:, q, :],
@@ -279,7 +279,7 @@ def tile_dynamicmemorybank_pa_kernel(tc, x, memory, w1, b1, out):
             copy = nc.scalar.copy if u == 0 else nc.vector.tensor_copy
             copy(out=mem_t[:, SLOTS * u : SLOTS * (u + 1)], in_=mt[:].rearrange("p j r -> p (j r)"))
         for k in range(2):
-            for call in x_transposes(k, XT_BANK + k):
+            for call in x_transposes(k, (XT_BANK, ET_BANKS[0])[k]):
                 nc.tensor.transpose(*call)
             x_copy_out(nc.scalar.copy if k == 0 else nc.vector.tensor_copy, k)
 
@@ -325,7 +325,7 @@ def tile_dynamicmemorybank_pa_kernel(tc, x, memory, w1, b1, out):
                 transposes += e_transposes(et)
             if energy_tick:
                 first = (len(transposes) + 1) // 2
-                en = bank(EN_BANKS[tick % 2], [P, SLOTS], F32)
+                en = bank(EN_BANKS[tick % 3], [P, SLOTS], F32)
                 for t in range(4):
                     if t % 2 == 0:
                         for call in transposes[:first] if t == 0 else transposes[first:]:
@@ -350,9 +350,9 @@ def tile_dynamicmemorybank_pa_kernel(tc, x, memory, w1, b1, out):
                 recip_copy_out(rt)
 
             if not energy_tick:
-                banks = list(EN_BANKS) + [XT_BANK]
+                banks = [XT_BANK] + [EN_BANKS[i % 3] for i in range(NT - 3, NT)]
                 if tick >= ATTENTION_DONE:
-                    banks += list(ET_BANKS) + [RT_BANK] + list(M2_BANKS)
+                    banks += list(ET_BANKS) + [RT_BANK, M2_BANK]
                 fuse((tick - NT) // NT, (tick - NT) % NT, banks, 2 if tick == last_tick else 1)
                 if m2 is not None:
                     retrieve(m2)

@@ -25,16 +25,22 @@ FLOPS = 2 * TOKENS * C * SLOTS * 2 + 2 * TOKENS * 2 * C * F
 
 EN_BANKS = (0, 1, 2)
 XT_BANK = 3
-ET_BANKS = (4, 5)
-RT_BANK = 6
-M2_BANK = 7
+ET_BANK = 4
+M2_BANKS = (5, 6)
+RT_BANK = 7
 
 XT_AT = -2
 ET_AT = 3
-RT_AT = 4
+EQ_AT = 5
 M2_AT = 7
-ATTENTION_DONE = NT + M2_AT
+RT_AT = 10
+RQ_AT = 11
+ATTENTION_DONE = NT + RT_AT - 1
 
+MEMQ_AT = 4
+XQ_AT = (7,11,13,17)
+WQ_AT = (9, 13, 25, 30)
+GATE_AT = (7, 9, 11, 13, 15, 17, 19, 21, 23, 25)
 W_PIECE = 256
 
 
@@ -82,6 +88,7 @@ def tile_dynamicmemorybank_pa_kernel(tc, x, memory, w1, b1, out):
         recip = keep.tile([P, NT], F32, name="recip")
         bias = keep.tile([P, F], BF16, name="bias")
         warm = keep.tile([P, 2], F32, name="warm")
+        gates = keep.tile([P, 16], F32, name="gates")
         w_sb = {}
         w_g = {}
         w_c = {}
@@ -106,14 +113,11 @@ def tile_dynamicmemorybank_pa_kernel(tc, x, memory, w1, b1, out):
         def load_w(g, h):
             cols = slice(h * HALF, (h + 1) * HALF)
             dst = w_sb[g, h][:].rearrange("p (t f) -> p t f", t=4)
-            if g == 0:
-                for u in range(2):
-                    nc.sync.dma_start(
-                        out=dst[:, 2 * u : 2 * u + 2, :],
-                        in_=w1[256 * u : 256 * u + 256, cols].rearrange("(q e) f -> q e f", e=2),
-                    )
-            else:
-                nc.sync.dma_start(out=dst, in_=w1[C : 2 * C, cols].rearrange("(p j) f -> p j f", j=4))
+            for u in range(2):
+                nc.sync.dma_start(
+                    out=dst[:, 2 * u : 2 * u + 2, :],
+                    in_=w1[C * g + 256 * u : C * g + 256 * u + 256, cols].rearrange("(q e) f -> q e f", e=2),
+                )
 
         nc.sync.dma_start(out=mem_sb[:].rearrange("p (j c) -> p j c", j=4), in_=mem_v)
         for n in range(4):
@@ -124,6 +128,7 @@ def tile_dynamicmemorybank_pa_kernel(tc, x, memory, w1, b1, out):
         xt_ps = {}
         et_ps = {}
         rt_ps = {}
+        r_sb = {}
         e_sb = {}
         e_g = {}
         e_c = {}
@@ -164,7 +169,7 @@ def tile_dynamicmemorybank_pa_kernel(tc, x, memory, w1, b1, out):
             )
 
         def e_transposes(k):
-            et_ps[k] = bank(ET_BANKS[k % 2], [P, 2, 4, P], BF16)
+            et_ps[k] = bank(ET_BANK, [P, 2, 4, P], BF16)
             return [
                 (et_ps[k][:, a, t, :], e_sb[2 * k + a][:, P * t : P * t + P], ident_b[:])
                 for a in range(2)
@@ -186,58 +191,61 @@ def tile_dynamicmemorybank_pa_kernel(tc, x, memory, w1, b1, out):
         def reciprocals(k):
             nc.vector.reciprocal(out=recip[:, 2 * k : 2 * k + 2], in_=rowsum[:, 2 * k : 2 * k + 2])
 
-        def recip_transposes(k):
-            rt_ps[k] = bank(RT_BANK, [P, 2, P], F32)
-            return [
-                (rt_ps[k][:, a, :], recip[:, 2 * k + a : 2 * k + a + 1].to_broadcast([P, P]), ident_f[:])
-                for a in range(2)
-            ]
-
-        def recip_copy_out(k):
-            r_b[k] = ring.tile([P, 2, P], F32, name="r_b", bufs=3)
-            nc.scalar.copy(out=r_b[k][:], in_=rt_ps[k][:])
-
         def retrieve(i):
             k, a = divmod(i, 2)
-            m2_ps[i] = bank(M2_BANK, [P, 4, P], F32)
-            for q in range(4):
-                nc.tensor.matmul_mx(
-                    out=m2_ps[i][:, q, :],
-                    lhsT=mem_c[:, P * q : P * q + P].bitcast(FP8X4),
-                    lhsT_scale=mem_s[:, P * q : P * q + P],
-                    rhs=e_c[k][:, P * a : P * a + P].bitcast(FP8X4),
-                    rhs_scale=e_s[k][:, P * a : P * a + P],
-                    start=True,
-                    stop=True,
-                )
+            m2_ps[i] = bank(M2_BANKS[i % 2], [P, C], F32)
+            nc.tensor.matmul_mx(
+                out=m2_ps[i][:],
+                lhsT=e_c[k][:, P * a : P * a + P].bitcast(FP8X4),
+                lhsT_scale=e_s[k][:, P * a : P * a + P],
+                rhs=mem_c[:].bitcast(FP8X4),
+                rhs_scale=mem_s[:],
+                start=True,
+                stop=True,
+            )
 
         def normalise(i):
-            k, a = divmod(i, 2)
-            if a == 0:
-                r_g[k] = ring.tile([P, 2 * P * 4], BF16, name="r_g", align_bytes=64)
-            nc.vector.tensor_tensor(
-                out=r_g[k][:].rearrange("p (a r q) -> p a r q", a=2, r=P, q=4)[:, a, :, :],
-                in0=m2_ps[i][:].rearrange("p q r -> p r q"),
-                in1=r_b[k][:, a, :].unsqueeze(2).to_broadcast([P, P, 4]),
-                op=ALU.mult,
+            r_sb[i] = ring.tile([P, C], BF16, name="r_sb", bufs=6)
+            nc.scalar.activation(out=r_sb[i][:], in_=m2_ps[i][:], func=ACT.Copy, scale=recip[:, i : i + 1])
+
+        def r_transposes(k):
+            rt_ps[k] = bank(RT_BANK, [P, 2, 2, P], F32)
+            return [
+                (rt_ps[k][:, a, u, :], r_sb[2 * k + a][:].bitcast(F32)[:, P * u : P * u + P], ident_f[:])
+                for a in range(2)
+                for u in range(2)
+            ]
+
+        def r_copy_out(k):
+            r_g[k] = ring.tile([P, 2 * P * 4], BF16, name="r_g", align_bytes=64)
+            nc.vector.tensor_copy(
+                out=r_g[k][:].bitcast(F32).rearrange("p (a r u) -> p a r u", a=2, r=P, u=2),
+                in_=rt_ps[k][:].rearrange("p a u r -> p a r u"),
             )
 
         def r_quantise(k):
             cols = slice(2 * P * k, 2 * P * (k + 1))
             nc.vector.quantize_mx(out=r_c[:, cols].bitcast(FP8X4), scales=r_s[:, cols], in_=r_g[k][:])
 
+        def gpsimd_copy(out, in_, one):
+            nc.gpsimd.tensor_scalar(out=out, in0=in_, scalar1=one, scalar2=0.0, op0=ALU.mult, op1=ALU.add)
+
         def mem_regroup():
-            nc.vector.tensor_copy(
-                out=mem_g[:].rearrange("p (q m j) -> p q m j", q=4, m=P, j=4),
-                in_=mem_sb[:].rearrange("p (j m q) -> p q m j", j=4, m=P, q=4),
+            gpsimd_copy(
+                mem_g[:].rearrange("p (c j) -> p c j", j=4), mem_sb[:].rearrange("p (j c) -> p c j", j=4), 1.0
             )
 
-        def w_regroup(copy, g, h, piece):
+        def w_regroup(g, h, piece, one):
             cols = slice(W_PIECE * piece, W_PIECE * (piece + 1))
-            copy(
-                out=w_g[g, h][:].rearrange("p (f t) -> p f t", t=4)[:, cols, :].rearrange("p (c i) t -> p c t i", i=4),
-                in_=w_sb[g, h][:].rearrange("p (t f) -> p t f", t=4)[:, :, cols].rearrange("p t (c i) -> p c t i", i=4),
+            gpsimd_copy(
+                w_g[g, h][:].rearrange("p (f t) -> p f t", t=4)[:, cols, :],
+                w_sb[g, h][:].rearrange("p (t f) -> p f t", t=4)[:, cols, :],
+                one,
             )
+
+        def gate(n):
+            nc.vector.memset(gates[:, n : n + 1], 1.0)
+            return gates[:, n : n + 1]
 
         def w_quantise(g, h):
             nc.vector.quantize_mx(out=w_c[g, h][:].bitcast(FP8X4), scales=w_s[g, h][:], in_=w_g[g, h][:])
@@ -279,56 +287,66 @@ def tile_dynamicmemorybank_pa_kernel(tc, x, memory, w1, b1, out):
             copy = nc.scalar.copy if u == 0 else nc.vector.tensor_copy
             copy(out=mem_t[:, SLOTS * u : SLOTS * (u + 1)], in_=mt[:].rearrange("p j r -> p (j r)"))
         for k in range(2):
-            for call in x_transposes(k, (XT_BANK, ET_BANKS[0])[k]):
+            for call in x_transposes(k, (XT_BANK, RT_BANK)[k]):
                 nc.tensor.transpose(*call)
             x_copy_out(nc.scalar.copy if k == 0 else nc.vector.tensor_copy, k)
 
         last_tick = NT + 2 * NT - 1
+        pieces = [(g, h, n) for g, h in ((1, 0), (0, 1), (1, 1)) for n in range(4)]
         for tick in range(last_tick + 1):
             energy_tick = tick < NT
             xt = pair_due(tick, XT_AT, 2)
             et = pair_due(tick, ET_AT)
+            eq = pair_due(tick, EQ_AT)
             rt = pair_due(tick, RT_AT)
+            rq = pair_due(tick, RQ_AT)
             m2 = tick - M2_AT if 0 <= tick - M2_AT < NT else None
 
-            if pair_due(tick, ET_AT + 1) is not None:
-                e_copy_out(pair_due(tick, ET_AT + 1))
             if tick == NT:
                 nc.scalar.activation(out=warm[:, 0:1], in_=warm[:, 1:2], func=ACT.Silu)
-            if tick % 2 == 1 and 7 <= tick <= 21:
-                w_regroup(nc.scalar.copy, (tick - 7) // 8, 1, (tick - 7) // 2 % 4)
-
-            if tick % 4 == 2 and energy_tick:
-                x_quantise(tick // 4)
-            if tick == ET_AT + 2:
-                nc.vector.quantize_mx(out=mem_c[:].bitcast(FP8X4), scales=mem_s[:], in_=mem_g[:])
-            if pair_due(tick, RT_AT - 1) is not None:
-                reciprocals(pair_due(tick, RT_AT - 1))
-            if pair_due(tick, M2_AT + 2) is not None:
-                r_quantise(pair_due(tick, M2_AT + 2))
-            for g in range(2):
-                if tick == 4 * g + 7:
-                    w_quantise(g, 0)
-                if tick == 8 * g + 16:
-                    w_quantise(g, 1)
             if tick == 0:
                 mem_regroup()
-            if 1 <= tick <= 8:
-                w_regroup(nc.vector.tensor_copy, (tick - 1) // 4, 0, (tick - 1) % 4)
+                for n in range(4):
+                    w_regroup(0, 0, n, 1.0)
+                for g, h, n in pieces[:2]:
+                    w_regroup(g, h, n, 1.0)
+                pieces = pieces[2:]
 
-            transposes = []
+            if pair_due(tick, ET_AT) is not None:
+                reciprocals(et)
+            if tick == MEMQ_AT:
+                nc.vector.quantize_mx(out=mem_c[:].bitcast(FP8X4), scales=mem_s[:], in_=mem_g[:])
+            if eq is not None:
+                e_quantise(eq)
+            if rq is not None:
+                r_quantise(rq)
+            if tick in XQ_AT:
+                x_quantise(XQ_AT.index(tick))
+            if tick in WQ_AT:
+                n = WQ_AT.index(tick)
+                w_quantise(n % 2, n // 2)
+            if tick in GATE_AT:
+                one = gate(GATE_AT.index(tick))
+                for g, h, n in pieces[:1] if tick != GATE_AT[-1] else pieces:
+                    w_regroup(g, h, n, one)
+                pieces = pieces[1:]
+
+            early = []
+            late = []
             if xt is not None:
-                transposes += x_transposes(xt, XT_BANK)
+                early += x_transposes(xt, XT_BANK)
             if rt is not None:
-                transposes += recip_transposes(rt)
+                early += r_transposes(rt)
             if et is not None:
-                transposes += e_transposes(et)
+                late += e_transposes(et)
             if energy_tick:
-                first = (len(transposes) + 1) // 2
                 en = bank(EN_BANKS[tick % 3], [P, SLOTS], F32)
                 for t in range(4):
-                    if t % 2 == 0:
-                        for call in transposes[:first] if t == 0 else transposes[first:]:
+                    if t == 0:
+                        for call in early:
+                            nc.tensor.transpose(*call)
+                    if t == 2:
+                        for call in late:
                             nc.tensor.transpose(*call)
                     if t == 1 and m2 is not None:
                         retrieve(m2)
@@ -341,23 +359,23 @@ def tile_dynamicmemorybank_pa_kernel(tc, x, memory, w1, b1, out):
                         stop=(t == 3),
                     )
             else:
-                for call in transposes:
+                for call in early + late:
                     nc.tensor.transpose(*call)
 
+            if et is not None:
+                e_copy_out(et)
             if xt is not None:
-                x_copy_out(nc.scalar.copy, xt)
+                x_copy_out(nc.scalar.copy if xt % 2 == 0 else nc.vector.tensor_copy, xt)
             if rt is not None:
-                recip_copy_out(rt)
+                r_copy_out(rt)
 
             if not energy_tick:
                 banks = [XT_BANK] + [EN_BANKS[i % 3] for i in range(NT - 3, NT)]
                 if tick >= ATTENTION_DONE:
-                    banks += list(ET_BANKS) + [RT_BANK, M2_BANK]
-                fuse((tick - NT) // NT, (tick - NT) % NT, banks, 2 if tick == last_tick else 1)
+                    banks += [ET_BANK, RT_BANK] + list(M2_BANKS)
                 if m2 is not None:
                     retrieve(m2)
                     normalise(m2)
-            if pair_due(tick, ET_AT + 2) is not None:
-                e_quantise(pair_due(tick, ET_AT + 2))
+                fuse((tick - NT) // NT, (tick - NT) % NT, banks, 2 if tick == last_tick else 1)
             if energy_tick:
                 energy_softmax_tail(tick, en)

@@ -37,6 +37,10 @@ RT_AT = 10
 RQ_AT = 11
 ATTENTION_DONE = NT + RT_AT - 1
 
+X_POS = 0
+R_POS = 0
+E_POS = 2
+M2_POS = 1
 MEMQ_AT = 4
 XQ_AT = (7,11,13,17)
 WQ_AT = (9, 13, 25, 30)
@@ -68,9 +72,7 @@ def tile_dynamicmemorybank_pa_kernel(tc, x, memory, w1, b1, out):
             return psum.tile(shape, dtype, tag="bank%d" % k, name="ps%d" % made[0])
 
         ident_f = keep.tile([P, P], F32, name="ident_f")
-        ident_b = keep.tile([P, P], BF16, name="ident_b")
         make_identity(nc, ident_f[:])
-        make_identity(nc, ident_b[:])
 
         mem_sb = keep.tile([P, 4 * C], BF16, name="mem_sb")
         mem_t = keep.tile([P, 2 * SLOTS], F32, name="mem_t")
@@ -105,9 +107,10 @@ def tile_dynamicmemorybank_pa_kernel(tc, x, memory, w1, b1, out):
         mem_values = mem_t[:].bitcast(BF16).rearrange("p (u c e) -> p u c e", u=2, e=2)
         mem_words = mem_sb[:].bitcast(F32).rearrange("p (j w) -> p j w", j=4)
 
-        def load_x(g):
+        def load_x(g, first=0, last=4):
             nc.sync.dma_start(
-                out=x_sb[g][:].rearrange("p (i c) -> p i c", i=4), in_=x_v[:, 4 * g : 4 * g + 4, :]
+                out=x_sb[g][:].rearrange("p (i c) -> p i c", i=4)[:, first:last, :],
+                in_=x_v[:, 4 * g + first : 4 * g + last, :],
             )
 
         def load_w(g, h):
@@ -119,10 +122,13 @@ def tile_dynamicmemorybank_pa_kernel(tc, x, memory, w1, b1, out):
                     in_=w1[C * g + 256 * u : C * g + 256 * u + 256, cols].rearrange("(q e) f -> q e f", e=2),
                 )
 
+        load_x(0, 0, 2)
         nc.sync.dma_start(out=mem_sb[:].rearrange("p (j c) -> p j c", j=4), in_=mem_v)
-        for n in range(4):
-            load_x(n)
+        load_x(0, 2, 4)
+        for n in range(3):
+            load_x(n + 1)
             load_w(n % 2, n // 2)
+        load_w(1, 1)
         nc.sync.dma_start(out=bias[:], in_=b1.partition_broadcast(P))
 
         xt_ps = {}
@@ -169,18 +175,18 @@ def tile_dynamicmemorybank_pa_kernel(tc, x, memory, w1, b1, out):
             )
 
         def e_transposes(k):
-            et_ps[k] = bank(ET_BANK, [P, 2, 4, P], BF16)
+            et_ps[k] = bank(ET_BANK, [P, 2, 2, P], F32)
             return [
-                (et_ps[k][:, a, t, :], e_sb[2 * k + a][:, P * t : P * t + P], ident_b[:])
+                (et_ps[k][:, a, u, :], e_sb[2 * k + a][:].bitcast(F32)[:, P * u : P * u + P], ident_f[:])
                 for a in range(2)
-                for t in range(4)
+                for u in range(2)
             ]
 
         def e_copy_out(k):
             e_g[k] = ring.tile([P, 2 * P * 4], BF16, name="e_g", align_bytes=64)
             nc.scalar.copy(
-                out=e_g[k][:].rearrange("p (a r t) -> p a r t", a=2, r=P, t=4),
-                in_=et_ps[k][:].rearrange("p a t r -> p a r t"),
+                out=e_g[k][:].bitcast(F32).rearrange("p (a r u) -> p a r u", a=2, r=P, u=2),
+                in_=et_ps[k][:].rearrange("p a u r -> p a r u"),
             )
 
         def e_quantise(k):
@@ -280,16 +286,24 @@ def tile_dynamicmemorybank_pa_kernel(tc, x, memory, w1, b1, out):
 
         nc.vector.memset(warm[:], 0.0)
         nc.scalar.activation(out=warm[:, 0:1], in_=warm[:, 1:2], func=ACT.Exp)
-        for u in range(2):
-            mt = bank(EN_BANKS[u], [P, 4, P], F32)
-            for j in range(4):
-                nc.tensor.transpose(mt[:, j, :], mem_words[:, j, P * u : P * u + P], ident_f[:])
-            copy = nc.scalar.copy if u == 0 else nc.vector.tensor_copy
-            copy(out=mem_t[:, SLOTS * u : SLOTS * (u + 1)], in_=mt[:].rearrange("p j r -> p (j r)"))
-        for k in range(2):
-            for call in x_transposes(k, (XT_BANK, RT_BANK)[k]):
+        copies = (nc.scalar.copy, nc.vector.tensor_copy)
+
+        def x_first(k, b, copy):
+            for call in x_transposes(k, b):
                 nc.tensor.transpose(*call)
-            x_copy_out(nc.scalar.copy if k == 0 else nc.vector.tensor_copy, k)
+            x_copy_out(copy, k)
+
+        x_first(0, XT_BANK, nc.scalar.copy)
+        for u in range(2):
+            for v in range(2):
+                mt = bank((EN_BANKS[0], EN_BANKS[1], ET_BANK, M2_BANKS[0])[2 * u + v], [P, 2, P], F32)
+                for e in range(2):
+                    nc.tensor.transpose(mt[:, e, :], mem_words[:, 2 * v + e, P * u : P * u + P], ident_f[:])
+                lo = SLOTS * u + 2 * P * v
+                copies[v](
+                    out=mem_t[:, lo : lo + 2 * P].rearrange("p (r e) -> p r e", e=2), in_=mt[:].rearrange("p e r -> p r e")
+                )
+        x_first(1, RT_BANK, nc.vector.tensor_copy)
 
         last_tick = NT + 2 * NT - 1
         pieces = [(g, h, n) for g, h in ((1, 0), (0, 1), (1, 1)) for n in range(4)]
@@ -331,24 +345,22 @@ def tile_dynamicmemorybank_pa_kernel(tc, x, memory, w1, b1, out):
                     w_regroup(g, h, n, one)
                 pieces = pieces[1:]
 
-            early = []
-            late = []
-            if xt is not None:
-                early += x_transposes(xt, XT_BANK)
-            if rt is not None:
-                early += r_transposes(rt)
-            if et is not None:
-                late += e_transposes(et)
+            xcalls = x_transposes(xt, XT_BANK) if xt is not None else []
+            rcalls = r_transposes(rt) if rt is not None else []
+            ecalls = e_transposes(et) if et is not None else []
             if energy_tick:
                 en = bank(EN_BANKS[tick % 3], [P, SLOTS], F32)
                 for t in range(4):
-                    if t == 0:
-                        for call in early:
+                    if t == X_POS:
+                        for call in xcalls:
                             nc.tensor.transpose(*call)
-                    if t == 2:
-                        for call in late:
+                    if t == R_POS:
+                        for call in rcalls:
                             nc.tensor.transpose(*call)
-                    if t == 1 and m2 is not None:
+                    if t == E_POS:
+                        for call in ecalls:
+                            nc.tensor.transpose(*call)
+                    if t == M2_POS and m2 is not None:
                         retrieve(m2)
                         normalise(m2)
                     nc.tensor.matmul(
@@ -359,7 +371,7 @@ def tile_dynamicmemorybank_pa_kernel(tc, x, memory, w1, b1, out):
                         stop=(t == 3),
                     )
             else:
-                for call in early + late:
+                for call in xcalls + rcalls + ecalls:
                     nc.tensor.transpose(*call)
 
             if et is not None:

@@ -41,11 +41,15 @@ X_POS = 0
 R_POS = 0
 E_POS = 2
 M2_POS = 1
+LAST = ((512, 256, 256), (512, 256, 256))
 MEMQ_AT = 4
-XQ_AT = (7,11,13,17)
-WQ_AT = (9, 13, 25, 30)
-GATE_AT = (7, 9, 11, 13, 15, 17, 19, 21, 23, 25)
-W_PIECE = 256
+XQ_AT = (3,7,11,15)
+WQ_AT = (9, 13, 19, 23)
+GATE_AT = (7, 9, 11, 13, 15, 17, 19, 21)
+GATE_N = (3, 3, 3, 3, 3, 3, 3, 3)
+NPIECE = 8
+UNG = 8
+W_PIECE = 128
 
 
 def pair_due(tick, offset, first=0):
@@ -258,14 +262,16 @@ def tile_dynamicmemorybank_pa_kernel(tc, x, memory, w1, b1, out):
 
         used = [0]
 
-        def fuse(h, i, banks, stores):
+        def fuse(h, i, banks, widths, silu_widths):
             v = ring.tile([P, HALF], F32, name="v", bufs=6)
             toks = slice(P * i, P * (i + 1))
-            for fc in range(HALF // BANK):
-                acc = bank(banks[used[0] % len(banks)], [P, BANK], F32)
+            lo = 0
+            done = 0
+            silu_widths = list(silu_widths)
+            for width in widths:
+                acc = bank(banks[used[0] % len(banks)], [P, width], F32)
                 used[0] += 1
-                lo, hi = BANK * fc, BANK * (fc + 1)
-                cols = slice(lo, hi)
+                cols = slice(lo, lo + width)
                 for g, codes, scales in ((0, x_c, x_s), (1, r_c, r_s)):
                     nc.tensor.matmul_mx(
                         out=acc[:],
@@ -277,12 +283,14 @@ def tile_dynamicmemorybank_pa_kernel(tc, x, memory, w1, b1, out):
                         stop=(g == 1),
                     )
                 nc.vector.tensor_tensor(
-                    out=v[:, cols], in0=acc[:], in1=bias[:, h * HALF + lo : h * HALF + hi], op=ALU.add
+                    out=v[:, cols], in0=acc[:], in1=bias[:, h * HALF + lo : h * HALF + lo + width], op=ALU.add
                 )
-                if stores == 2 or hi == HALF:
-                    lo = lo if stores == 2 else 0
-                    nc.scalar.activation(out=v[:, lo:hi], in_=v[:, lo:hi], func=ACT.Silu)
-                    nc.sync.dma_start(out=out_v[:, i, h * HALF + lo : h * HALF + hi], in_=v[:, lo:hi])
+                lo += width
+                if lo == done + silu_widths[0]:
+                    nc.scalar.activation(out=v[:, done:lo], in_=v[:, done:lo], func=ACT.Silu)
+                    nc.sync.dma_start(out=out_v[:, i, h * HALF + done : h * HALF + lo], in_=v[:, done:lo])
+                    done = lo
+                    silu_widths.pop(0)
 
         nc.vector.memset(warm[:], 0.0)
         nc.scalar.activation(out=warm[:, 0:1], in_=warm[:, 1:2], func=ACT.Exp)
@@ -306,7 +314,7 @@ def tile_dynamicmemorybank_pa_kernel(tc, x, memory, w1, b1, out):
         x_first(1, RT_BANK, nc.vector.tensor_copy)
 
         last_tick = NT + 2 * NT - 1
-        pieces = [(g, h, n) for g, h in ((1, 0), (0, 1), (1, 1)) for n in range(4)]
+        pieces = [(g, h, n) for g, h in ((0, 0), (1, 0), (0, 1), (1, 1)) for n in range(NPIECE)]
         for tick in range(last_tick + 1):
             energy_tick = tick < NT
             xt = pair_due(tick, XT_AT, 2)
@@ -320,11 +328,9 @@ def tile_dynamicmemorybank_pa_kernel(tc, x, memory, w1, b1, out):
                 nc.scalar.activation(out=warm[:, 0:1], in_=warm[:, 1:2], func=ACT.Silu)
             if tick == 0:
                 mem_regroup()
-                for n in range(4):
-                    w_regroup(0, 0, n, 1.0)
-                for g, h, n in pieces[:2]:
+                for g, h, n in pieces[:UNG]:
                     w_regroup(g, h, n, 1.0)
-                pieces = pieces[2:]
+                pieces = pieces[UNG:]
 
             if pair_due(tick, ET_AT) is not None:
                 reciprocals(et)
@@ -341,9 +347,10 @@ def tile_dynamicmemorybank_pa_kernel(tc, x, memory, w1, b1, out):
                 w_quantise(n % 2, n // 2)
             if tick in GATE_AT:
                 one = gate(GATE_AT.index(tick))
-                for g, h, n in pieces[:1] if tick != GATE_AT[-1] else pieces:
-                    w_regroup(g, h, n, one)
-                pieces = pieces[1:]
+                n = GATE_N[GATE_AT.index(tick)]
+                for g, h, n2 in pieces[:n]:
+                    w_regroup(g, h, n2, one)
+                pieces = pieces[n:]
 
             xcalls = x_transposes(xt, XT_BANK) if xt is not None else []
             rcalls = r_transposes(rt) if rt is not None else []
@@ -377,7 +384,7 @@ def tile_dynamicmemorybank_pa_kernel(tc, x, memory, w1, b1, out):
             if et is not None:
                 e_copy_out(et)
             if xt is not None:
-                x_copy_out(nc.scalar.copy if xt % 2 == 0 else nc.vector.tensor_copy, xt)
+                x_copy_out(nc.scalar.copy, xt)
             if rt is not None:
                 r_copy_out(rt)
 
@@ -388,6 +395,7 @@ def tile_dynamicmemorybank_pa_kernel(tc, x, memory, w1, b1, out):
                 if m2 is not None:
                     retrieve(m2)
                     normalise(m2)
-                fuse((tick - NT) // NT, (tick - NT) % NT, banks, 2 if tick == last_tick else 1)
+                widths, silu_widths = LAST if tick == last_tick else ((BANK, BANK), (HALF,))
+                fuse((tick - NT) // NT, (tick - NT) % NT, banks, widths, silu_widths)
             if energy_tick:
                 energy_softmax_tail(tick, en)

@@ -263,7 +263,7 @@ def tile_dynamicmemorybank_pa_kernel(tc, x, memory, w1, b1, out):
         used = [0]
 
         def fuse(h, i, banks, widths, silu_widths):
-            v = ring.tile([P, HALF], F32, name="v", bufs=6)
+            v = ring.tile([P, HALF], F32, name="v", bufs=10)
             toks = slice(P * i, P * (i + 1))
             lo = 0
             done = 0

@@ -29,7 +29,7 @@ ET_BANK = 4
 M2_BANKS = (5, 6)
 RT_BANK = 7
 
-XT_AT = -2
+XT_AT = -3
 ET_AT = 3
 EQ_AT = 5
 M2_AT = 7
@@ -37,14 +37,16 @@ RT_AT = 10
 RQ_AT = 11
 ATTENTION_DONE = NT + RT_AT - 1
 
-X_POS = 0
-R_POS = 0
+X_POS = 2
+R_POS = 2
 E_POS = 2
 M2_POS = 1
+CHUNK = 256
+WQ_N = 2
+WQ0 = 5
+XQ_LAG = -1
 LAST = ((512, 256, 256), (512, 256, 256))
 MEMQ_AT = 4
-XQ_AT = (3,7,11,15)
-WQ_AT = (9, 13, 19, 23)
 GATE_AT = (7, 9, 11, 13, 15, 17, 19, 21)
 GATE_N = (3, 3, 3, 3, 3, 3, 3, 3)
 NPIECE = 8
@@ -160,10 +162,10 @@ def tile_dynamicmemorybank_pa_kernel(tc, x, memory, w1, b1, out):
         def x_copy_out(copy, k):
             copy(out=x_words[:, 2 * k : 2 * k + 2, :, :], in_=xt_ps[k][:].rearrange("p a u r -> p a r u"))
 
-        def x_quantise(g):
-            cols = slice(4 * P * g, 4 * P * (g + 1))
+        def x_quantise(k):
+            cols = slice(2 * P * k, 2 * P * (k + 1))
             nc.vector.quantize_mx(
-                out=x_c[:, cols].bitcast(FP8X4), scales=x_s[:, cols], in_=x_g[:, 16 * P * g : 16 * P * (g + 1)]
+                out=x_c[:, cols].bitcast(FP8X4), scales=x_s[:, cols], in_=x_g[:, 8 * P * k : 8 * P * (k + 1)]
             )
 
         def energy_softmax_tail(i, en):
@@ -237,6 +239,8 @@ def tile_dynamicmemorybank_pa_kernel(tc, x, memory, w1, b1, out):
             cols = slice(2 * P * k, 2 * P * (k + 1))
             nc.vector.quantize_mx(out=r_c[:, cols].bitcast(FP8X4), scales=r_s[:, cols], in_=r_g[k][:])
 
+        emitted = {}
+
         def gpsimd_copy(out, in_, one):
             nc.gpsimd.tensor_scalar(out=out, in0=in_, scalar1=one, scalar2=0.0, op0=ALU.mult, op1=ALU.add)
 
@@ -247,6 +251,7 @@ def tile_dynamicmemorybank_pa_kernel(tc, x, memory, w1, b1, out):
 
         def w_regroup(g, h, piece, one):
             cols = slice(W_PIECE * piece, W_PIECE * (piece + 1))
+            emitted[g, h] = emitted.get((g, h), 0) + 1
             gpsimd_copy(
                 w_g[g, h][:].rearrange("p (f t) -> p f t", t=4)[:, cols, :],
                 w_sb[g, h][:].rearrange("p (t f) -> p f t", t=4)[:, cols, :],
@@ -257,8 +262,12 @@ def tile_dynamicmemorybank_pa_kernel(tc, x, memory, w1, b1, out):
             nc.vector.memset(gates[:, n : n + 1], 1.0)
             return gates[:, n : n + 1]
 
-        def w_quantise(g, h):
-            nc.vector.quantize_mx(out=w_c[g, h][:].bitcast(FP8X4), scales=w_s[g, h][:], in_=w_g[g, h][:])
+        def w_quantise(g, h, c):
+            lo, hi = CHUNK * c, CHUNK * (c + 1)
+            assert emitted.get((g, h), 0) * W_PIECE >= hi
+            nc.vector.quantize_mx(
+                out=w_c[g, h][:, lo:hi].bitcast(FP8X4), scales=w_s[g, h][:, lo:hi], in_=w_g[g, h][:, 4 * lo : 4 * hi]
+            )
 
         used = [0]
 
@@ -314,6 +323,8 @@ def tile_dynamicmemorybank_pa_kernel(tc, x, memory, w1, b1, out):
         x_first(1, RT_BANK, nc.vector.tensor_copy)
 
         last_tick = NT + 2 * NT - 1
+        chunks = [(g, h, n) for g, h in ((0, 0), (1, 0), (0, 1), (1, 1)) for n in range(HALF // CHUNK)]
+        ready = []
         pieces = [(g, h, n) for g, h in ((0, 0), (1, 0), (0, 1), (1, 1)) for n in range(NPIECE)]
         for tick in range(last_tick + 1):
             energy_tick = tick < NT
@@ -340,11 +351,14 @@ def tile_dynamicmemorybank_pa_kernel(tc, x, memory, w1, b1, out):
                 e_quantise(eq)
             if rq is not None:
                 r_quantise(rq)
-            if tick in XQ_AT:
-                x_quantise(XQ_AT.index(tick))
-            if tick in WQ_AT:
-                n = WQ_AT.index(tick)
-                w_quantise(n % 2, n // 2)
+            for k in range(NPAIR):
+                if tick == max(1, 2 * k + XQ_LAG):
+                    x_quantise(k)
+            if tick % 2 == 1:
+                for g, h, c in [q for q in chunks if q in ready][:WQ_N]:
+                    w_quantise(g, h, c)
+                    chunks.remove((g, h, c))
+                ready = [q for q in chunks if emitted.get((q[0], q[1]), 0) * W_PIECE >= CHUNK * (q[2] + 1)] if tick >= WQ0 else []
             if tick in GATE_AT:
                 one = gate(GATE_AT.index(tick))
                 n = GATE_N[GATE_AT.index(tick)]

@@ -47,11 +47,11 @@ WQ0 = 5
 XQ_LAG = -1
 LAST = ((512, 256, 256), (512, 256, 256))
 MEMQ_AT = 4
-GATE_AT = (7, 9, 11, 13, 15, 17, 19, 21)
-GATE_N = (3, 3, 3, 3, 3, 3, 3, 3)
-NPIECE = 8
-UNG = 8
-W_PIECE = 128
+GATE_AT = (5, 7, 9, 11, 13, 15, 17, 19, 21, 23, 25, 27)
+GATE_N = (1, 1, 1, 1, 1, 1, 1, 1, 1, 1, 1, 1)
+NPIECE = 4
+UNG = 4
+W_PIECE = 256
 
 
 def pair_due(tick, offset, first=0):

@@ -81,7 +81,7 @@ def tile_dynamicmemorybank_pa_kernel(tc, x, memory, w1, b1, out):
         make_identity(nc, ident_f[:])
 
         mem_sb = keep.tile([P, 4 * C], BF16, name="mem_sb")
-        mem_t = keep.tile([P, 2 * SLOTS], F32, name="mem_t")
+        mem_t = keep.tile([P, 4 * SLOTS], BF16, name="mem_t")
         mem_g = keep.tile([P, 4 * C], BF16, name="mem_g", align_bytes=64)
         mem_c = keep.tile([P, C], U32, name="mem_c", align_bytes=64)
         mem_s = keep.tile([P, C], U8, name="mem_s", align_bytes=64)
@@ -110,7 +110,7 @@ def tile_dynamicmemorybank_pa_kernel(tc, x, memory, w1, b1, out):
 
         x_words = x_g[:].bitcast(F32).rearrange("p (i r u) -> p i r u", i=NT, r=P, u=2)
         x_values = x_g[:].rearrange("p (i r t) -> p i r t", i=NT, r=P, t=4)
-        mem_values = mem_t[:].bitcast(BF16).rearrange("p (u c e) -> p u c e", u=2, e=2)
+        mem_values = mem_t[:].rearrange("p (u e c) -> p u e c", u=2, e=2)
         mem_words = mem_sb[:].bitcast(F32).rearrange("p (j w) -> p j w", j=4)
 
         def load_x(g, first=0, last=4):
@@ -316,10 +316,11 @@ def tile_dynamicmemorybank_pa_kernel(tc, x, memory, w1, b1, out):
                 mt = bank((EN_BANKS[0], EN_BANKS[1], ET_BANK, M2_BANKS[0])[2 * u + v], [P, 2, P], F32)
                 for e in range(2):
                     nc.tensor.transpose(mt[:, e, :], mem_words[:, 2 * v + e, P * u : P * u + P], ident_f[:])
-                lo = SLOTS * u + 2 * P * v
-                copies[v](
-                    out=mem_t[:, lo : lo + 2 * P].rearrange("p (r e) -> p r e", e=2), in_=mt[:].rearrange("p e r -> p r e")
-                )
+                for c in range(2):
+                    copies[v](
+                        out=mem_values[:, u, c, 2 * P * v : 2 * P * (v + 1)].rearrange("p (r e) -> p r e", e=2),
+                        in_=mt[:].bitcast(BF16).rearrange("p e (r c) -> p c r e", c=2)[:, c, :, :],
+                    )
         x_first(1, RT_BANK, nc.vector.tensor_copy)
 
         last_tick = NT + 2 * NT - 1
@@ -387,7 +388,7 @@ def tile_dynamicmemorybank_pa_kernel(tc, x, memory, w1, b1, out):
                     nc.tensor.matmul(
                         out=en[:],
                         lhsT=x_values[:, tick, :, t],
-                        rhs=mem_values[:, t // 2, :, t % 2],
+                        rhs=mem_values[:, t // 2, t % 2, :],
                         start=(t == 0),
                         stop=(t == 3),
                     )

@@ -45,6 +45,7 @@ CHUNK = 256
 WQ_N = 2
 WQ0 = 5
 XQ_LAG = -1
+BUSY = (7, 2)
 LAST = ((512, 256, 256), (512, 256, 256))
 MEMQ_AT = 4
 GATE_AT = (5, 7, 9, 11, 13, 15, 17, 19, 21, 23, 25, 27)
@@ -310,7 +311,17 @@ def tile_dynamicmemorybank_pa_kernel(tc, x, memory, w1, b1, out):
                 nc.tensor.transpose(*call)
             x_copy_out(copy, k)
 
+        idle = keep.tile([P, BANK], BF16, name="idle")
+        nc.vector.memset(idle[:], 0.0)
+        unread = bank(M2_BANKS[1], [P, BANK], F32)
+
+        def keep_busy(count):
+            for n in range(count):
+                nc.tensor.matmul(out=unread[:], lhsT=idle[:, 0:P], rhs=idle[:], start=True, stop=True)
+
+        keep_busy(BUSY[0])
         x_first(0, XT_BANK, nc.scalar.copy)
+        keep_busy(BUSY[1])
         for u in range(2):
             for v in range(2):
                 mt = bank((EN_BANKS[0], EN_BANKS[1], ET_BANK, M2_BANKS[0])[2 * u + v], [P, 2, P], F32)

@@ -37,15 +37,15 @@ RT_AT = 10
 RQ_AT = 11
 ATTENTION_DONE = NT + RT_AT - 1
 
-X_POS = 2
-R_POS = 2
-E_POS = 2
+X_POS = 3
+R_POS = 3
+E_POS = 3
 M2_POS = 1
 CHUNK = 256
 WQ_N = 2
 WQ0 = 5
-XQ_LAG = -1
-BUSY = (7, 2)
+XQ_LAG = 5
+BUSY = (7, 2, 1)
 LAST = ((512, 256, 256), (512, 256, 256))
 MEMQ_AT = 4
 GATE_AT = (5, 7, 9, 11, 13, 15, 17, 19, 21, 23, 25, 27)
@@ -333,6 +333,7 @@ def tile_dynamicmemorybank_pa_kernel(tc, x, memory, w1, b1, out):
                         in_=mt[:].bitcast(BF16).rearrange("p e (r c) -> p c r e", c=2)[:, c, :, :],
                     )
         x_first(1, RT_BANK, nc.vector.tensor_copy)
+        keep_busy(BUSY[2])
 
         last_tick = NT + 2 * NT - 1
         chunks = [(g, h, n) for g, h in ((0, 0), (1, 0), (0, 1), (1, 1)) for n in range(HALF // CHUNK)]
@@ -364,7 +365,7 @@ def tile_dynamicmemorybank_pa_kernel(tc, x, memory, w1, b1, out):
             if rq is not None:
                 r_quantise(rq)
             for k in range(NPAIR):
-                if tick == max(1, 2 * k + XQ_LAG):
+                if tick == 2 * k + XQ_LAG:
                     x_quantise(k)
             if tick % 2 == 1:
                 for g, h, c in [q for q in chunks if q in ready][:WQ_N]:

from contextlib import ExitStack

import concourse.mybir as mybir
from concourse.masks import make_identity

F32 = mybir.dt.float32
BF16 = mybir.dt.bfloat16
U32 = mybir.dt.uint32
U8 = mybir.dt.uint8
FP8X4 = mybir.dt.float8_e4m3fn_x4
ACT = mybir.ActivationFunctionType
ALU = mybir.AluOpType
AX = mybir.AxisListType

P = 128
TOKENS = 2048
C = 512
SLOTS = 512
F = 2048
NT = TOKENS // P
NPAIR = NT // 2
HALF = F // 2
BANK = 512
FLOPS = 2 * TOKENS * C * SLOTS * 2 + 2 * TOKENS * 2 * C * F

EN_BANKS = (0, 1, 2)
XT_BANK = 3
ET_BANK = 4
M2_BANKS = (5, 6)
RT_BANK = 7

XT_AT = -3
ET_AT = 3
EQ_AT = 5
M2_AT = 7
RT_AT = 10
RQ_AT = 11
ATTENTION_DONE = NT + RT_AT - 1

X_POS = 3
R_POS = 3
E_POS = 3
M2_POS = 1
CHUNK = 256
WQ_N = 2
WQ0 = 5
XQ_LAG = 5
BUSY = (7, 2, 1)
LAST = ((512, 256, 256), (512, 256, 256))
MEMQ_AT = 4
GATE_AT = (5, 7, 9, 11, 13, 15, 17, 19, 21, 23, 25, 27)
GATE_N = (1, 1, 1, 1, 1, 1, 1, 1, 1, 1, 1, 1)
NPIECE = 4
UNG = 4
W_PIECE = 256


def pair_due(tick, offset, first=0):
    k, odd = divmod(tick - offset, 2)
    return k if odd == 0 and first <= k < NPAIR else None


def tile_dynamicmemorybank_pa_kernel(tc, x, memory, w1, b1, out):
    nc = tc.nc
    with ExitStack() as ctx:
        keep = ctx.enter_context(tc.tile_pool(name="keep", bufs=1))
        ring = ctx.enter_context(tc.tile_pool(name="ring", bufs=2))
        psum = ctx.enter_context(tc.psum_pool(name="psum", bufs=1))
        ctx.enter_context(tc.manual_schedule())

        x_v = x.flatten_outer_dims().rearrange("(p i) c -> p i c", i=NT)
        out_v = out.flatten_outer_dims().rearrange("(p i) f -> p i f", i=NT)
        mem_v = memory.flatten_outer_dims().rearrange("(p j) c -> p j c", j=4)

        made = [0]

        def bank(k, shape, dtype):
            made[0] += 1
            return psum.tile(shape, dtype, tag="bank%d" % k, name="ps%d" % made[0])

        ident_f = keep.tile([P, P], F32, name="ident_f")
        make_identity(nc, ident_f[:])

        mem_sb = keep.tile([P, 4 * C], BF16, name="mem_sb")
        mem_t = keep.tile([P, 4 * SLOTS], BF16, name="mem_t")
        mem_g = keep.tile([P, 4 * C], BF16, name="mem_g", align_bytes=64)
        mem_c = keep.tile([P, C], U32, name="mem_c", align_bytes=64)
        mem_s = keep.tile([P, C], U8, name="mem_s", align_bytes=64)
        x_sb = [keep.tile([P, 4 * C], BF16, name="x_sb%d" % g) for g in range(4)]
        x_g = keep.tile([P, NT * P * 4], BF16, name="x_g", align_bytes=64)
        x_c = keep.tile([P, TOKENS], U32, name="x_c", align_bytes=64)
        x_s = keep.tile([P, TOKENS], U8, name="x_s", align_bytes=64)
        r_c = keep.tile([P, TOKENS], U32, name="r_c", align_bytes=64)
        r_s = keep.tile([P, TOKENS], U8, name="r_s", align_bytes=64)
        negmax = keep.tile([P, NT], F32, name="negmax")
        rowsum = keep.tile([P, NT], F32, name="rowsum")
        recip = keep.tile([P, NT], F32, name="recip")
        bias = keep.tile([P, F], BF16, name="bias")
        warm = keep.tile([P, 2], F32, name="warm")
        gates = keep.tile([P, 16], F32, name="gates")
        w_sb = {}
        w_g = {}
        w_c = {}
        w_s = {}
        for h in range(2):
            for g in range(2):
                w_sb[g, h] = keep.tile([P, 4 * HALF], BF16, name="w_sb%d%d" % (g, h))
                w_g[g, h] = keep.tile([P, 4 * HALF], BF16, name="w_g%d%d" % (g, h), align_bytes=64)
                w_c[g, h] = keep.tile([P, HALF], U32, name="w_c%d%d" % (g, h), align_bytes=64)
                w_s[g, h] = keep.tile([P, HALF], U8, name="w_s%d%d" % (g, h), align_bytes=64)

        x_words = x_g[:].bitcast(F32).rearrange("p (i r u) -> p i r u", i=NT, r=P, u=2)
        x_values = x_g[:].rearrange("p (i r t) -> p i r t", i=NT, r=P, t=4)
        mem_values = mem_t[:].rearrange("p (u e c) -> p u e c", u=2, e=2)
        mem_words = mem_sb[:].bitcast(F32).rearrange("p (j w) -> p j w", j=4)

        def load_x(g, first=0, last=4):
            nc.sync.dma_start(
                out=x_sb[g][:].rearrange("p (i c) -> p i c", i=4)[:, first:last, :],
                in_=x_v[:, 4 * g + first : 4 * g + last, :],
            )

        def load_w(g, h):
            cols = slice(h * HALF, (h + 1) * HALF)
            dst = w_sb[g, h][:].rearrange("p (t f) -> p t f", t=4)
            for u in range(2):
                nc.sync.dma_start(
                    out=dst[:, 2 * u : 2 * u + 2, :],
                    in_=w1[C * g + 256 * u : C * g + 256 * u + 256, cols].rearrange("(q e) f -> q e f", e=2),
                )

        load_x(0, 0, 2)
        nc.sync.dma_start(out=mem_sb[:].rearrange("p (j c) -> p j c", j=4), in_=mem_v)
        load_x(0, 2, 4)
        for n in range(3):
            load_x(n + 1)
            load_w(n % 2, n // 2)
        load_w(1, 1)
        nc.sync.dma_start(out=bias[:], in_=b1.partition_broadcast(P))

        xt_ps = {}
        et_ps = {}
        rt_ps = {}
        r_sb = {}
        e_sb = {}
        e_g = {}
        e_c = {}
        e_s = {}
        r_b = {}
        r_g = {}
        m2_ps = {}

        def x_transposes(k, b):
            xt_ps[k] = bank(b, [P, 2, 2, P], F32)
            calls = []
            for a in range(2):
                i = 2 * k + a
                words = x_sb[i // 4][:].bitcast(F32).rearrange("p (i w) -> p i w", i=4)
                for u in range(2):
                    calls.append((xt_ps[k][:, a, u, :], words[:, i % 4, P * u : P * u + P], ident_f[:]))
            return calls

        def x_copy_out(copy, k):
            copy(out=x_words[:, 2 * k : 2 * k + 2, :, :], in_=xt_ps[k][:].rearrange("p a u r -> p a r u"))

        def x_quantise(k):
            cols = slice(2 * P * k, 2 * P * (k + 1))
            nc.vector.quantize_mx(
                out=x_c[:, cols].bitcast(FP8X4), scales=x_s[:, cols], in_=x_g[:, 8 * P * k : 8 * P * (k + 1)]
            )

        def energy_softmax_tail(i, en):
            nc.vector.tensor_reduce(out=negmax[:, i : i + 1], in_=en[:], axis=AX.X, op=ALU.max, negate=True)
            e_sb[i] = ring.tile([P, SLOTS], BF16, name="e_sb", bufs=6)
            nc.scalar.activation(
                out=e_sb[i][:],
                in_=en[:],
                func=ACT.Exp,
                bias=negmax[:, i : i + 1],
                scale=1.0,
                accum_out=rowsum[:, i : i + 1],
            )

        def e_transposes(k):
            et_ps[k] = bank(ET_BANK, [P, 2, 2, P], F32)
            return [
                (et_ps[k][:, a, u, :], e_sb[2 * k + a][:].bitcast(F32)[:, P * u : P * u + P], ident_f[:])
                for a in range(2)
                for u in range(2)
            ]

        def e_copy_out(k):
            e_g[k] = ring.tile([P, 2 * P * 4], BF16, name="e_g", align_bytes=64)
            nc.scalar.copy(
                out=e_g[k][:].bitcast(F32).rearrange("p (a r u) -> p a r u", a=2, r=P, u=2),
                in_=et_ps[k][:].rearrange("p a u r -> p a r u"),
            )

        def e_quantise(k):
            e_c[k] = ring.tile([P, 2 * P], U32, name="e_c", align_bytes=64)
            e_s[k] = ring.tile([P, 2 * P], U8, name="e_s", align_bytes=64)
            nc.vector.quantize_mx(out=e_c[k][:].bitcast(FP8X4), scales=e_s[k][:], in_=e_g[k][:])

        def reciprocals(k):
            nc.vector.reciprocal(out=recip[:, 2 * k : 2 * k + 2], in_=rowsum[:, 2 * k : 2 * k + 2])

        def retrieve(i):
            k, a = divmod(i, 2)
            m2_ps[i] = bank(M2_BANKS[i % 2], [P, C], F32)
            nc.tensor.matmul_mx(
                out=m2_ps[i][:],
                lhsT=e_c[k][:, P * a : P * a + P].bitcast(FP8X4),
                lhsT_scale=e_s[k][:, P * a : P * a + P],
                rhs=mem_c[:].bitcast(FP8X4),
                rhs_scale=mem_s[:],
                start=True,
                stop=True,
            )

        def normalise(i):
            r_sb[i] = ring.tile([P, C], BF16, name="r_sb", bufs=6)
            nc.scalar.activation(out=r_sb[i][:], in_=m2_ps[i][:], func=ACT.Copy, scale=recip[:, i : i + 1])

        def r_transposes(k):
            rt_ps[k] = bank(RT_BANK, [P, 2, 2, P], F32)
            return [
                (rt_ps[k][:, a, u, :], r_sb[2 * k + a][:].bitcast(F32)[:, P * u : P * u + P], ident_f[:])
                for a in range(2)
                for u in range(2)
            ]

        def r_copy_out(k):
            r_g[k] = ring.tile([P, 2 * P * 4], BF16, name="r_g", align_bytes=64)
            nc.vector.tensor_copy(
                out=r_g[k][:].bitcast(F32).rearrange("p (a r u) -> p a r u", a=2, r=P, u=2),
                in_=rt_ps[k][:].rearrange("p a u r -> p a r u"),
            )

        def r_quantise(k):
            cols = slice(2 * P * k, 2 * P * (k + 1))
            nc.vector.quantize_mx(out=r_c[:, cols].bitcast(FP8X4), scales=r_s[:, cols], in_=r_g[k][:])

        emitted = {}

        def gpsimd_copy(out, in_, one):
            nc.gpsimd.tensor_scalar(out=out, in0=in_, scalar1=one, scalar2=0.0, op0=ALU.mult, op1=ALU.add)

        def mem_regroup():
            gpsimd_copy(
                mem_g[:].rearrange("p (c j) -> p c j", j=4), mem_sb[:].rearrange("p (j c) -> p c j", j=4), 1.0
            )

        def w_regroup(g, h, piece, one):
            cols = slice(W_PIECE * piece, W_PIECE * (piece + 1))
            emitted[g, h] = emitted.get((g, h), 0) + 1
            gpsimd_copy(
                w_g[g, h][:].rearrange("p (f t) -> p f t", t=4)[:, cols, :],
                w_sb[g, h][:].rearrange("p (t f) -> p f t", t=4)[:, cols, :],
                one,
            )

        def gate(n):
            nc.vector.memset(gates[:, n : n + 1], 1.0)
            return gates[:, n : n + 1]

        def w_quantise(g, h, c):
            lo, hi = CHUNK * c, CHUNK * (c + 1)
            assert emitted.get((g, h), 0) * W_PIECE >= hi
            nc.vector.quantize_mx(
                out=w_c[g, h][:, lo:hi].bitcast(FP8X4), scales=w_s[g, h][:, lo:hi], in_=w_g[g, h][:, 4 * lo : 4 * hi]
            )

        used = [0]

        def fuse(h, i, banks, widths, silu_widths):
            v = ring.tile([P, HALF], F32, name="v", bufs=10)
            toks = slice(P * i, P * (i + 1))
            lo = 0
            done = 0
            silu_widths = list(silu_widths)
            for width in widths:
                acc = bank(banks[used[0] % len(banks)], [P, width], F32)
                used[0] += 1
                cols = slice(lo, lo + width)
                for g, codes, scales in ((0, x_c, x_s), (1, r_c, r_s)):
                    nc.tensor.matmul_mx(
                        out=acc[:],
                        lhsT=codes[:, toks].bitcast(FP8X4),
                        lhsT_scale=scales[:, toks],
                        rhs=w_c[g, h][:, cols].bitcast(FP8X4),
                        rhs_scale=w_s[g, h][:, cols],
                        start=(g == 0),
                        stop=(g == 1),
                    )
                nc.vector.tensor_tensor(
                    out=v[:, cols], in0=acc[:], in1=bias[:, h * HALF + lo : h * HALF + lo + width], op=ALU.add
                )
                lo += width
                if lo == done + silu_widths[0]:
                    nc.scalar.activation(out=v[:, done:lo], in_=v[:, done:lo], func=ACT.Silu)
                    nc.sync.dma_start(out=out_v[:, i, h * HALF + done : h * HALF + lo], in_=v[:, done:lo])
                    done = lo
                    silu_widths.pop(0)

        nc.vector.memset(warm[:], 0.0)
        nc.scalar.activation(out=warm[:, 0:1], in_=warm[:, 1:2], func=ACT.Exp)
        copies = (nc.scalar.copy, nc.vector.tensor_copy)

        def x_first(k, b, copy):
            for call in x_transposes(k, b):
                nc.tensor.transpose(*call)
            x_copy_out(copy, k)

        idle = keep.tile([P, BANK], BF16, name="idle")
        nc.vector.memset(idle[:], 0.0)
        unread = bank(M2_BANKS[1], [P, BANK], F32)

        def keep_busy(count):
            for n in range(count):
                nc.tensor.matmul(out=unread[:], lhsT=idle[:, 0:P], rhs=idle[:], start=True, stop=True)

        keep_busy(BUSY[0])
        x_first(0, XT_BANK, nc.scalar.copy)
        keep_busy(BUSY[1])
        for u in range(2):
            for v in range(2):
                mt = bank((EN_BANKS[0], EN_BANKS[1], ET_BANK, M2_BANKS[0])[2 * u + v], [P, 2, P], F32)
                for e in range(2):
                    nc.tensor.transpose(mt[:, e, :], mem_words[:, 2 * v + e, P * u : P * u + P], ident_f[:])
                for c in range(2):
                    copies[v](
                        out=mem_values[:, u, c, 2 * P * v : 2 * P * (v + 1)].rearrange("p (r e) -> p r e", e=2),
                        in_=mt[:].bitcast(BF16).rearrange("p e (r c) -> p c r e", c=2)[:, c, :, :],
                    )
        x_first(1, RT_BANK, nc.vector.tensor_copy)
        keep_busy(BUSY[2])

        last_tick = NT + 2 * NT - 1
        chunks = [(g, h, n) for g, h in ((0, 0), (1, 0), (0, 1), (1, 1)) for n in range(HALF // CHUNK)]
        ready = []
        pieces = [(g, h, n) for g, h in ((0, 0), (1, 0), (0, 1), (1, 1)) for n in range(NPIECE)]
        for tick in range(last_tick + 1):
            energy_tick = tick < NT
            xt = pair_due(tick, XT_AT, 2)
            et = pair_due(tick, ET_AT)
            eq = pair_due(tick, EQ_AT)
            rt = pair_due(tick, RT_AT)
            rq = pair_due(tick, RQ_AT)
            m2 = tick - M2_AT if 0 <= tick - M2_AT < NT else None

            if tick == NT:
                nc.scalar.activation(out=warm[:, 0:1], in_=warm[:, 1:2], func=ACT.Silu)
            if tick == 0:
                mem_regroup()
                for g, h, n in pieces[:UNG]:
                    w_regroup(g, h, n, 1.0)
                pieces = pieces[UNG:]

            if pair_due(tick, ET_AT) is not None:
                reciprocals(et)
            if tick == MEMQ_AT:
                nc.vector.quantize_mx(out=mem_c[:].bitcast(FP8X4), scales=mem_s[:], in_=mem_g[:])
            if eq is not None:
                e_quantise(eq)
            if rq is not None:
                r_quantise(rq)
            for k in range(NPAIR):
                if tick == 2 * k + XQ_LAG:
                    x_quantise(k)
            if tick % 2 == 1:
                for g, h, c in [q for q in chunks if q in ready][:WQ_N]:
                    w_quantise(g, h, c)
                    chunks.remove((g, h, c))
                ready = [q for q in chunks if emitted.get((q[0], q[1]), 0) * W_PIECE >= CHUNK * (q[2] + 1)] if tick >= WQ0 else []
            if tick in GATE_AT:
                one = gate(GATE_AT.index(tick))
                n = GATE_N[GATE_AT.index(tick)]
                for g, h, n2 in pieces[:n]:
                    w_regroup(g, h, n2, one)
                pieces = pieces[n:]

            xcalls = x_transposes(xt, XT_BANK) if xt is not None else []
            rcalls = r_transposes(rt) if rt is not None else []
            ecalls = e_transposes(et) if et is not None else []
            if energy_tick:
                en = bank(EN_BANKS[tick % 3], [P, SLOTS], F32)
                for t in range(4):
                    if t == X_POS:
                        for call in xcalls:
                            nc.tensor.transpose(*call)
                    if t == R_POS:
                        for call in rcalls:
                            nc.tensor.transpose(*call)
                    if t == E_POS:
                        for call in ecalls:
                            nc.tensor.transpose(*call)
                    if t == M2_POS and m2 is not None:
                        retrieve(m2)
                        normalise(m2)
                    nc.tensor.matmul(
                        out=en[:],
                        lhsT=x_values[:, tick, :, t],
                        rhs=mem_values[:, t // 2, t % 2, :],
                        start=(t == 0),
                        stop=(t == 3),
                    )
            else:
                for call in xcalls + rcalls + ecalls:
                    nc.tensor.transpose(*call)

            if et is not None:
                e_copy_out(et)
            if xt is not None:
                x_copy_out(nc.scalar.copy, xt)
            if rt is not None:
                r_copy_out(rt)

            if not energy_tick:
                banks = [XT_BANK] + [EN_BANKS[i % 3] for i in range(NT - 3, NT)]
                if tick >= ATTENTION_DONE:
                    banks += [ET_BANK, RT_BANK] + list(M2_BANKS)
                if m2 is not None:
                    retrieve(m2)
                    normalise(m2)
                widths, silu_widths = LAST if tick == last_tick else ((BANK, BANK), (HALF,))
                fuse((tick - NT) // NT, (tick - NT) % NT, banks, widths, silu_widths)
            if energy_tick:
                energy_softmax_tail(tick, en)
